import numpy as np
import ml_dtypes


def mxq(x, axis, fmt="e4m3"):
    dtype, down = {"e4m3": (ml_dtypes.float8_e4m3fn, 7), "e5m2": (ml_dtypes.float8_e5m2, 14)}[fmt]
    v = np.moveaxis(np.asarray(x, np.float32).astype(ml_dtypes.bfloat16).astype(np.float64), axis, -1)
    blocks = v.reshape(v.shape[:-1] + (-1, 32))
    amax = np.abs(blocks).max(-1, keepdims=True)
    byte = np.maximum(np.where(amax > 0, np.frexp(amax)[1] - 1 + 127, 0) - down, 1)
    scale = np.exp2(byte - 127.0)
    codes = (blocks / scale).astype(np.float32).astype(dtype).astype(np.float64)
    return np.moveaxis((codes * scale).reshape(v.shape), -1, axis)


WIDE = False


def mx_kscale(k):
    if not WIDE:
        return np.ones(k)
    levels = np.array([10, -10, 5, -5, 0])
    a = np.random.permutation(np.resize(levels, k // 512 * 4)).reshape(k // 512, 4)
    idx = np.arange(k)
    return np.exp2(a[idx // 512, idx % 128 // 32])


BF16 = ml_dtypes.bfloat16


def bf(x):
    return np.asarray(x, np.float32).astype(BF16)


def f64(x):
    return np.asarray(x).astype(np.float64)


B, L, D, DV, BN = 8, 1024, 1024, 256, 128
SV = 2.0 * B / np.sqrt(L)
SB = 2.0 * B / L


def setup_inputs():
    s, u = mx_kscale(D), mx_kscale(D)
    return {"qp_top": bf(np.random.standard_normal((B, BN, D)) * s),
            "kp": bf(np.random.standard_normal((B, L, D)) / s),
            "v": bf(np.random.standard_normal((B, L, D)) * u),
            "Wv": bf(np.random.standard_normal((DV, D)) * SV / np.sqrt(D) / u[None, :]),
            "bv": bf(np.random.standard_normal(DV) * SB)}


def reference(qp_top, kp, v, Wv, bv):
    vp = (mxq(f64(v), 2, "e4m3") @ mxq(f64(Wv), 1, "e4m3").T) + f64(bv)
    score = (mxq(f64(qp_top), 2, "e4m3") @ mxq(f64(kp), 2, "e4m3").transpose(0, 2, 1)) * (1.0 / np.sqrt(D))
    e = np.exp(score - score.max(0, keepdims=True))
    attn = e / e.sum(0, keepdims=True)
    return mxq(attn, 2, "e4m3") @ mxq(vp, 1, "e4m3")

@@ -1,0 +1,306 @@
+from contextlib import ExitStack
+
+import concourse.mybir as mybir
+from concourse.masks import make_identity
+
+F32 = mybir.dt.float32
+BF16 = mybir.dt.bfloat16
+U32 = mybir.dt.uint32
+U8 = mybir.dt.uint8
+FP8X4 = mybir.dt.float8_e4m3fn_x4
+ALU = mybir.AluOpType
+ACT = mybir.ActivationFunctionType
+AX = mybir.AxisListType
+
+B, L, D, DV, BN = 8, 1024, 1024, 256, 128
+P = 128
+FLOPS = 2 * B * L * D * DV + 2 * B * BN * L * D + 2 * B * BN * L * DV
+
+PINNED = False
+RAW_BUFS = 10
+AHEAD = 3
+W_STEP = 8
+GP_MUL = False
+GP_TREE = False
+V_EVAC_HEAD = 3
+V_EVAC_TAIL = 0
+
+
+def tile_bottleneck_attention_pa_t_kernel(tc, qp_top, kp, v, Wv, bv, out):
+    nc = tc.nc
+    with ExitStack() as ctx:
+        const = ctx.enter_context(tc.tile_pool(name="const", bufs=1))
+        rawp = ctx.enter_context(tc.tile_pool(name="rawp", bufs=RAW_BUFS))
+        grpp = ctx.enter_context(tc.tile_pool(name="grpp", bufs=3))
+        codp = ctx.enter_context(tc.tile_pool(name="codp", bufs=3))
+        smp = ctx.enter_context(tc.tile_pool(name="smp", bufs=2))
+        atp = ctx.enter_context(tc.tile_pool(name="atp", bufs=3))
+        vpp = ctx.enter_context(tc.tile_pool(name="vpp", bufs=4))
+        otp = ctx.enter_context(tc.tile_pool(name="otp", bufs=B))
+        xtp = ctx.enter_context(tc.psum_pool(name="xtp", bufs=4))
+        accp = ctx.enter_context(tc.psum_pool(name="accp", bufs=4))
+        if PINNED:
+            ctx.enter_context(tc.manual_schedule())
+
+        ident = const.tile([P, P], F32, name="ident")
+        make_identity(nc, ident[:])
+        qcod = const.tile([P, 2048], U32, name="qcod", align_bytes=64)
+        qsca = const.tile([P, 2048], U8, name="qsca", align_bytes=64)
+        wraw = const.tile([P, 2048], BF16, name="wraw")
+        wgrp = const.tile([P, 2048], BF16, name="wgrp", align_bytes=64)
+        wcod = const.tile([P, 512], U32, name="wcod", align_bytes=64)
+        wsca = const.tile([P, 512], U8, name="wsca", align_bytes=64)
+        bias = const.tile([P, DV], BF16, name="bias")
+        ex = const.tile([P, 8192], F32, name="ex")
+        ssum = const.tile([P, 1024], F32, name="ssum")
+        rcp = const.tile([P, 1024], F32, name="rcp")
+
+        qview = qp_top.rearrange("b i d -> i b d")
+        kview = kp.rearrange("b (g p t) d -> g t p b d", g=2, p=P, t=4)
+        vview = v.rearrange("b (g p t) d -> b g p t d", g=2, p=P, t=4)
+
+        seq = [("q", 0, 0), ("k", 0, 0), ("q", 1, 0), ("k", 0, 1)]
+        seq.extend([("k", u, h) for u in range(1, 8) for h in range(2)])
+        seq.extend([("v", b, g) for b in range(B) for g in range(2)])
+        N = len(seq)
+
+        raws, xts, grps, cods, scas, accs = {}, {}, {}, {}, {}, {}
+        sm = {}
+
+        def load(n):
+            kind, a, h = seq[n]
+            if kind == "q":
+                src = qview[:, 4 * a : 4 * a + 4, :]
+            elif kind == "k":
+                src = kview[a // 4, a % 4][:, 4 * h : 4 * h + 4, :]
+            else:
+                src = vview[a, h]
+            raw = rawp.tile([P, 4096], BF16, name="raw", tag="raw")
+            nc.sync.dma_start(out=raw[:].rearrange("p (s d) -> p s d", s=4), in_=src)
+            raws[n] = raw
+
+        def flip_slab(words, s):
+            xt = xtp.tile([P, 512], F32, name="xt", tag="xt")
+            for q in range(4):
+                lo = 512 * s + 128 * q
+                nc.tensor.transpose(xt[:, 128 * q : 128 * q + 128], words[:, lo : lo + 128], ident[:])
+            return xt
+
+        def evac_slab(eng_is_vector, gf, xt, s):
+            dst = gf[:, 512 * s : 512 * s + 512].rearrange("p (c r u) -> p c r u", c=2, r=P, u=2)
+            src = xt[:].rearrange("p (c u r) -> p c r u", c=2, u=2, r=P)
+            if eng_is_vector:
+                nc.vector.tensor_copy(out=dst, in_=src)
+            else:
+                nc.scalar.copy(out=dst, in_=src)
+
+        def flip(n):
+            words = raws[n][:].bitcast(F32)
+            xts[n] = [flip_slab(words, s) for s in range(4)]
+            if n + RAW_BUFS < N:
+                load(n + RAW_BUFS)
+
+        def evac(n):
+            grp = grpp.tile([P, 4096], BF16, name="grp", tag="grp", align_bytes=64)
+            gf = grp[:].bitcast(F32)
+            for s in range(4):
+                on_vector = (n < V_EVAC_HEAD or n >= N - V_EVAC_TAIL) and s >= 2
+                evac_slab(on_vector, gf, xts[n][s], s)
+            grps[n] = grp
+
+        def quant(n):
+            kind, a, h = seq[n]
+            if kind == "q":
+                cod = qcod[:, 1024 * a : 1024 * a + 1024]
+                sca = qsca[:, 1024 * a : 1024 * a + 1024]
+            else:
+                codt = codp.tile([P, 1024], U32, name="codt", tag="codt", align_bytes=64)
+                scat = codp.tile([P, 1024], U8, name="scat", tag="scat", align_bytes=64)
+                cod = codt[:]
+                sca = scat[:]
+            nc.vector.quantize_mx(out=cod.bitcast(FP8X4), scales=sca, in_=grps[n][:])
+            cods[n] = cod
+            scas[n] = sca
+
+        def mx(acc, lc, ls, lo, rc, rs, ro, width, c):
+            nc.tensor.matmul_mx(
+                out=acc,
+                lhsT=lc[:, lo : lo + P].bitcast(FP8X4),
+                lhsT_scale=ls[:, lo : lo + P],
+                rhs=rc[:, ro : ro + width].bitcast(FP8X4),
+                rhs_scale=rs[:, ro : ro + width],
+                start=(c == 0),
+                stop=(c == 1),
+            )
+
+        def passes_k(n):
+            kind, u, h = seq[n]
+            sc = accp.tile([P, 512], F32, name="sc", tag="acc")
+            for s in range(4):
+                b = 4 * h + s
+                for c in range(2):
+                    mx(sc[:, P * s : P * s + P], cods[n], scas[n], (2 * s + c) * P,
+                       qcod, qsca, (2 * b + c) * P, P, c)
+            accs[("k", u, h)] = sc
+
+        def passes_v(n):
+            kind, b, g = seq[n]
+            for h in range(2):
+                vb = accp.tile([P, 512], F32, name="vb", tag="acc")
+                for t in range(4):
+                    for c in range(2):
+                        mx(vb[:, P * t : P * t + P], cods[n], scas[n], (2 * t + c) * P,
+                           wcod, wsca, (2 * h + c) * P, P, c)
+                accs[("v", n, h)] = vb
+
+        def half_max(u, h):
+            mh = smp.tile([P, P], F32, name="mh%d" % h, tag="mh%d" % h)
+            nc.vector.tensor_reduce(
+                out=mh[:], in_=accs[("k", u, h)][:].rearrange("p (b i) -> p i b", b=4),
+                axis=AX.X, op=ALU.max)
+            sm[("mh", u, h)] = mh
+
+        def comb(u):
+            m = smp.tile([P, P], F32, name="m", tag="m")
+            nc.vector.tensor_tensor(out=m[:], in0=sm[("mh", u, 0)][:], in1=sm[("mh", u, 1)][:], op=ALU.max)
+            sm[("m", u)] = m
+
+        def sub(u, h):
+            lo = 1024 * u + 512 * h
+            nc.vector.tensor_tensor(
+                out=ex[:, lo : lo + 512].rearrange("p (b i) -> p b i", b=4),
+                in0=accs[("k", u, h)][:].rearrange("p (b i) -> p b i", b=4),
+                in1=sm[("m", u)][:].unsqueeze(1).to_broadcast([P, 4, P]),
+                op=ALU.subtract)
+
+        def expo(u):
+            lo = 1024 * u
+            nc.scalar.activation(out=ex[:, lo : lo + 1024], in_=ex[:, lo : lo + 1024],
+                                 func=ACT.Exp, scale=1.0 / 32.0)
+
+        def adder():
+            return nc.gpsimd if GP_TREE else nc.vector
+
+        def tree1(u):
+            lo = 1024 * u
+            t1 = smp.tile([P, 512], F32, name="t1", tag="t1")
+            adder().tensor_tensor(out=t1[:], in0=ex[:, lo : lo + 512], in1=ex[:, lo + 512 : lo + 1024], op=ALU.add)
+            sm[("t1", u)] = t1
+
+        def tree2(u):
+            t1 = sm[("t1", u)]
+            t2 = smp.tile([P, 256], F32, name="t2", tag="t2")
+            adder().tensor_tensor(out=t2[:], in0=t1[:, 0:256], in1=t1[:, 256:512], op=ALU.add)
+            sm[("t2", u)] = t2
+
+        def tree3(u):
+            t2 = sm[("t2", u)]
+            adder().tensor_tensor(out=ssum[:, P * u : P * u + P], in0=t2[:, 0:P], in1=t2[:, P:256], op=ALU.add)
+
+        def recip(u):
+            nc.vector.reciprocal(out=rcp[:, P * u : P * u + P], in_=ssum[:, P * u : P * u + P])
+
+        def mul(b):
+            ag = atp.tile([P, 1024], BF16, name="ag", tag="ag", align_bytes=64)
+            eng = nc.gpsimd if GP_MUL else nc.vector
+            eng.tensor_tensor(
+                out=ag[:].rearrange("p (g i t) -> p g i t", g=2, i=P, t=4),
+                in0=ex[:].rearrange("p (g t b i) -> p b g i t", g=2, t=4, b=B, i=P)[:, b],
+                in1=rcp[:].rearrange("p (g t i) -> p g i t", g=2, t=4, i=P),
+                op=ALU.mult)
+            sm[("ag", b)] = ag
+
+        def quant_attn(b):
+            acod = atp.tile([P, 256], U32, name="acod", tag="acod", align_bytes=64)
+            asca = atp.tile([P, 256], U8, name="asca", tag="asca", align_bytes=64)
+            nc.vector.quantize_mx(out=acod[:].bitcast(FP8X4), scales=asca[:], in_=sm[("ag", b)][:])
+            sm[("acod", b)] = acod
+            sm[("asca", b)] = asca
+
+        def add_bias(n):
+            vg = vpp.tile([P, 1024], BF16, name="vg", tag="vg", align_bytes=64)
+            for h in range(2):
+                nc.vector.tensor_tensor(
+                    out=vg[:, 512 * h : 512 * h + 512].rearrange("p (n t) -> p n t", t=4),
+                    in0=accs[("v", n, h)][:].rearrange("p (t n) -> p n t", t=4),
+                    in1=bias[:, P * h : P * h + P].unsqueeze(2).to_broadcast([P, P, 4]),
+                    op=ALU.add)
+            sm[("vg", n)] = vg
+
+        def quant_vp(n):
+            pcod = vpp.tile([P, 256], U32, name="pcod", tag="pcod", align_bytes=64)
+            psca = vpp.tile([P, 256], U8, name="psca", tag="psca", align_bytes=64)
+            nc.vector.quantize_mx(out=pcod[:].bitcast(FP8X4), scales=psca[:], in_=sm[("vg", n)][:])
+            sm[("pcod", n)] = pcod
+            sm[("psca", n)] = psca
+
+        def passes_o(b, n1):
+            ob = accp.tile([P, 512], F32, name="ob", tag="acc")
+            for g in range(2):
+                n = n1 - 1 + g
+                mx(ob[:, 0:DV], sm[("acod", b)], sm[("asca", b)], P * g,
+                   sm[("pcod", n)], sm[("psca", n)], 0, DV, g)
+            accs[("o", b)] = ob
+
+        def finish(b):
+            ot = otp.tile([P, DV], F32, name="ot", tag="ot")
+            nc.scalar.copy(out=ot[:], in_=accs[("o", b)][:, 0:DV])
+            nc.sync.dma_start(out=out[b], in_=ot[:])
+
+        def w_flip():
+            words = wraw[:].bitcast(F32)
+            xts["w"] = [flip_slab(words, s) for s in range(2)]
+
+        def w_evac():
+            gf = wgrp[:].bitcast(F32)
+            for s in range(2):
+                evac_slab(False, gf, xts["w"][s], s)
+
+        def w_quant():
+            nc.vector.quantize_mx(out=wcod[:].bitcast(FP8X4), scales=wsca[:], in_=wgrp[:])
+
+        plan = {}
+
+        def at(step, slot, fn, *args):
+            plan[(step, slot)] = plan.get((step, slot), []) + [(fn, args)]
+
+        for n in range(N):
+            kind, a, h = seq[n]
+            at(n - AHEAD, 0, flip, n)
+            at(n - AHEAD, 20, evac, n)
+            at(n, 10, quant, n)
+            if kind == "k":
+                at(n, 30, passes_k, n)
+                if h == 1:
+                    at(n, 61, half_max, a, 0)
+                    at(n + 1, 40, half_max, a, 1)
+                    at(n + 1, 42, comb, a)
+                    at(n + 1, 44, sub, a, 0)
+                    at(n + 1, 44, sub, a, 1)
+                    at(n + 1, 50, expo, a)
+                    at(n + 2, 60, tree1, a)
+                    at(n + 2, 62, tree2, a)
+                    at(n + 3, 41, tree3, a)
+                    at(n + 3, 43, recip, a)
+            if kind == "v":
+                at(n, 30, passes_v, n)
+                at(n + 1, 25, add_bias, n)
+                at(n + 2, 60, quant_vp, n)
+                if h == 1:
+                    at(n + 1, 63, mul, a)
+                    at(n + 2, 64, quant_attn, a)
+                    at(n + 3, 45, passes_o, a, n)
+                    at(n + 3, 50, finish, a)
+        at(W_STEP, 1, w_flip)
+        at(W_STEP, 21, w_evac)
+        at(W_STEP + 1, 11, w_quant)
+
+        for n in range(min(RAW_BUFS, N)):
+            load(n)
+            if n == 3:
+                nc.sync.dma_start(out=wraw[:].rearrange("p (h d) -> p h d", h=2),
+                                  in_=Wv.rearrange("(h p) d -> p h d", p=P))
+                nc.sync.dma_start(out=bias[:], in_=bv.partition_broadcast(P))
+        for key in sorted(plan):
+            for fn, args in plan[key]:
+                fn(*args)

@@ -17,13 +17,19 @@ P = 128
 FLOPS = 2 * B * L * D * DV + 2 * B * BN * L * D + 2 * B * BN * L * DV
 
 PINNED = False
-RAW_BUFS = 10
+RAW_BUFS = 8
 AHEAD = 3
+RAMP = 0
 W_STEP = 8
-GP_MUL = False
-GP_TREE = False
+PE_SUM = True
 V_EVAC_HEAD = 3
 V_EVAC_TAIL = 0
+EXP_AT = [1,2,3,4]
+SUM_AT = 5
+RCP_AT = 6
+BACK_AT = 7
+MUL_AT = [8,8,9,9]
+QA_AT = 10
 
 
 def tile_bottleneck_attention_pa_t_kernel(tc, qp_top, kp, v, Wv, bv, out):
@@ -33,12 +39,13 @@ def tile_bottleneck_attention_pa_t_kernel(tc, qp_top, kp, v, Wv, bv, out):
         rawp = ctx.enter_context(tc.tile_pool(name="rawp", bufs=RAW_BUFS))
         grpp = ctx.enter_context(tc.tile_pool(name="grpp", bufs=3))
         codp = ctx.enter_context(tc.tile_pool(name="codp", bufs=3))
+        dep = ctx.enter_context(tc.tile_pool(name="dep", bufs=3))
         smp = ctx.enter_context(tc.tile_pool(name="smp", bufs=2))
-        atp = ctx.enter_context(tc.tile_pool(name="atp", bufs=3))
-        vpp = ctx.enter_context(tc.tile_pool(name="vpp", bufs=4))
-        otp = ctx.enter_context(tc.tile_pool(name="otp", bufs=B))
+        vpp = ctx.enter_context(tc.tile_pool(name="vpp", bufs=3))
+        otp = ctx.enter_context(tc.tile_pool(name="otp", bufs=4))
         xtp = ctx.enter_context(tc.psum_pool(name="xtp", bufs=4))
-        accp = ctx.enter_context(tc.psum_pool(name="accp", bufs=4))
+        accp = ctx.enter_context(tc.psum_pool(name="accp", bufs=3))
+        mscp = ctx.enter_context(tc.psum_pool(name="mscp", bufs=1))
         if PINNED:
             ctx.enter_context(tc.manual_schedule())
 
@@ -51,9 +58,11 @@ def tile_bottleneck_attention_pa_t_kernel(tc, qp_top, kp, v, Wv, bv, out):
         wcod = const.tile([P, 512], U32, name="wcod", align_bytes=64)
         wsca = const.tile([P, 512], U8, name="wsca", align_bytes=64)
         bias = const.tile([P, DV], BF16, name="bias")
-        ex = const.tile([P, 8192], F32, name="ex")
-        ssum = const.tile([P, 1024], F32, name="ssum")
-        rcp = const.tile([P, 1024], F32, name="rcp")
+        pcod = const.tile([P, 4096], U32, name="pcod", align_bytes=64)
+        psca = const.tile([P, 4096], U8, name="psca", align_bytes=64)
+        acod = const.tile([P, 2048], U32, name="acod", align_bytes=64)
+        asca = const.tile([P, 2048], U8, name="asca", align_bytes=64)
+        ag = const.tile([P, 4096], BF16, name="ag", align_bytes=64)
 
         qview = qp_top.rearrange("b i d -> i b d")
         kview = kp.rearrange("b (g p t) d -> g t p b d", g=2, p=P, t=4)
@@ -166,56 +175,56 @@ def tile_bottleneck_attention_pa_t_kernel(tc, qp_top, kp, v, Wv, bv, out):
             sm[("m", u)] = m
 
         def sub(u, h):
-            lo = 1024 * u + 512 * h
+            g, t = u // 4, u % 4
+            if ("d", g) not in sm:
+                dg = dep.tile([P, 4096], F32, name="dg", tag="de")
+                sm[("d", g)] = dg
+            lo = 1024 * t + 512 * h
             nc.vector.tensor_tensor(
-                out=ex[:, lo : lo + 512].rearrange("p (b i) -> p b i", b=4),
+                out=sm[("d", g)][:, lo : lo + 512].rearrange("p (b i) -> p b i", b=4),
                 in0=accs[("k", u, h)][:].rearrange("p (b i) -> p b i", b=4),
                 in1=sm[("m", u)][:].unsqueeze(1).to_broadcast([P, 4, P]),
                 op=ALU.subtract)
 
-        def expo(u):
-            lo = 1024 * u
-            nc.scalar.activation(out=ex[:, lo : lo + 1024], in_=ex[:, lo : lo + 1024],
-                                 func=ACT.Exp, scale=1.0 / 32.0)
+        def expo(g, x):
+            if ("e", g) not in sm:
+                eg = dep.tile([P, 4096], F32, name="eg", tag="de")
+                sm[("e", g)] = eg
+            nc.scalar.activation(
+                out=sm[("e", g)][:, 1024 * x : 1024 * x + 1024].rearrange("p (b i t) -> p b i t", b=2, i=P, t=4),
+                in_=sm[("d", g)][:].rearrange("p (t b i) -> p b i t", t=4, b=B, i=P)[:, 2 * x : 2 * x + 2],
+                func=ACT.Exp, scale=1.0 / 32.0)
 
-        def adder():
-            return nc.gpsimd if GP_TREE else nc.vector
+        def sum_pe(g):
+            sb = mscp.tile([P, 512], F32, name="sb", tag="msc")
+            eg = sm[("e", g)]
+            for k in range(4):
+                for b in range(B):
+                    nc.tensor.matmul(out=sb[:, P * k : P * k + P], lhsT=eg[:, 512 * b + P * k : 512 * b + P * k + P],
+                                     rhs=ident[:], is_transpose=True, start=(b == 0), stop=(b == B - 1))
+            sm[("sb", g)] = sb
 
-        def tree1(u):
-            lo = 1024 * u
-            t1 = smp.tile([P, 512], F32, name="t1", tag="t1")
-            adder().tensor_tensor(out=t1[:], in0=ex[:, lo : lo + 512], in1=ex[:, lo + 512 : lo + 1024], op=ALU.add)
-            sm[("t1", u)] = t1
+        def recip(g):
+            rt = smp.tile([P, 512], F32, name="rt", tag="rt")
+            nc.vector.reciprocal(out=rt[:], in_=sm[("sb", g)][:])
+            sm[("rt", g)] = rt
 
-        def tree2(u):
-            t1 = sm[("t1", u)]
-            t2 = smp.tile([P, 256], F32, name="t2", tag="t2")
-            adder().tensor_tensor(out=t2[:], in0=t1[:, 0:256], in1=t1[:, 256:512], op=ALU.add)
-            sm[("t2", u)] = t2
+        def back_pe(g):
+            rb = mscp.tile([P, 512], F32, name="rb", tag="msc")
+            for k in range(4):
+                nc.tensor.transpose(rb[:, P * k : P * k + P], sm[("rt", g)][:, P * k : P * k + P], ident[:])
+            sm[("rb", g)] = rb
 
-        def tree3(u):
-            t2 = sm[("t2", u)]
-            adder().tensor_tensor(out=ssum[:, P * u : P * u + P], in0=t2[:, 0:P], in1=t2[:, P:256], op=ALU.add)
-
-        def recip(u):
-            nc.vector.reciprocal(out=rcp[:, P * u : P * u + P], in_=ssum[:, P * u : P * u + P])
-
-        def mul(b):
-            ag = atp.tile([P, 1024], BF16, name="ag", tag="ag", align_bytes=64)
-            eng = nc.gpsimd if GP_MUL else nc.vector
-            eng.tensor_tensor(
-                out=ag[:].rearrange("p (g i t) -> p g i t", g=2, i=P, t=4),
-                in0=ex[:].rearrange("p (g t b i) -> p b g i t", g=2, t=4, b=B, i=P)[:, b],
-                in1=rcp[:].rearrange("p (g t i) -> p g i t", g=2, t=4, i=P),
+        def mul(g, x):
+            nc.vector.tensor_tensor(
+                out=ag[:, 1024 * x : 1024 * x + 1024].rearrange("p (b c) -> p b c", b=2),
+                in0=sm[("e", g)][:, 1024 * x : 1024 * x + 1024].rearrange("p (b c) -> p b c", b=2),
+                in1=sm[("rb", g)][:].unsqueeze(1).to_broadcast([P, 2, 512]),
                 op=ALU.mult)
-            sm[("ag", b)] = ag
 
-        def quant_attn(b):
-            acod = atp.tile([P, 256], U32, name="acod", tag="acod", align_bytes=64)
-            asca = atp.tile([P, 256], U8, name="asca", tag="asca", align_bytes=64)
-            nc.vector.quantize_mx(out=acod[:].bitcast(FP8X4), scales=asca[:], in_=sm[("ag", b)][:])
-            sm[("acod", b)] = acod
-            sm[("asca", b)] = asca
+        def quant_attn(g):
+            nc.vector.quantize_mx(out=acod[:, 1024 * g : 1024 * g + 1024].bitcast(FP8X4),
+                                  scales=asca[:, 1024 * g : 1024 * g + 1024], in_=ag[:])
 
         def add_bias(n):
             vg = vpp.tile([P, 1024], BF16, name="vg", tag="vg", align_bytes=64)
@@ -228,18 +237,15 @@ def tile_bottleneck_attention_pa_t_kernel(tc, qp_top, kp, v, Wv, bv, out):
             sm[("vg", n)] = vg
 
         def quant_vp(n):
-            pcod = vpp.tile([P, 256], U32, name="pcod", tag="pcod", align_bytes=64)
-            psca = vpp.tile([P, 256], U8, name="psca", tag="psca", align_bytes=64)
-            nc.vector.quantize_mx(out=pcod[:].bitcast(FP8X4), scales=psca[:], in_=sm[("vg", n)][:])
-            sm[("pcod", n)] = pcod
-            sm[("psca", n)] = psca
+            kind, b, g = seq[n]
+            lo = 256 * (2 * b + g)
+            nc.vector.quantize_mx(out=pcod[:, lo : lo + 256].bitcast(FP8X4), scales=psca[:, lo : lo + 256],
+                                  in_=sm[("vg", n)][:])
 
-        def passes_o(b, n1):
-            ob = accp.tile([P, 512], F32, name="ob", tag="acc")
+        def passes_o(b):
+            ob = mscp.tile([P, 512], F32, name="ob", tag="msc")
             for g in range(2):
-                n = n1 - 1 + g
-                mx(ob[:, 0:DV], sm[("acod", b)], sm[("asca", b)], P * g,
-                   sm[("pcod", n)], sm[("psca", n)], 0, DV, g)
+                mx(ob[:, 0:DV], acod, asca, 1024 * g + P * b, pcod, psca, 256 * (2 * b + g), DV, g)
             accs[("o", b)] = ob
 
         def finish(b):
@@ -264,10 +270,12 @@ def tile_bottleneck_attention_pa_t_kernel(tc, qp_top, kp, v, Wv, bv, out):
         def at(step, slot, fn, *args):
             plan[(step, slot)] = plan.get((step, slot), []) + [(fn, args)]
 
+        qa_step = 0
         for n in range(N):
             kind, a, h = seq[n]
-            at(n - AHEAD, 0, flip, n)
-            at(n - AHEAD, 20, evac, n)
+            ahead = min(AHEAD, 1 + n // RAMP) if RAMP else AHEAD
+            at(n - ahead, 0, flip, n)
+            at(n - ahead, 20, evac, n)
             at(n, 10, quant, n)
             if kind == "k":
                 at(n, 30, passes_k, n)
@@ -277,20 +285,28 @@ def tile_bottleneck_attention_pa_t_kernel(tc, qp_top, kp, v, Wv, bv, out):
                     at(n + 1, 42, comb, a)
                     at(n + 1, 44, sub, a, 0)
                     at(n + 1, 44, sub, a, 1)
-                    at(n + 1, 50, expo, a)
-                    at(n + 2, 60, tree1, a)
-                    at(n + 2, 62, tree2, a)
-                    at(n + 3, 41, tree3, a)
-                    at(n + 3, 43, recip, a)
+                    if a % 4 == 3:
+                        g = a // 4
+                        for x in range(4):
+                            at(n + EXP_AT[x], 50, expo, g, x)
+                            at(n + MUL_AT[x], 63, mul, g, x)
+                        at(n + SUM_AT, 2, sum_pe, g)
+                        at(n + RCP_AT, 12, recip, g)
+                        at(n + BACK_AT, 2, back_pe, g)
+                        at(n + QA_AT, 64, quant_attn, g)
+                        qa_step = n + QA_AT
             if kind == "v":
                 at(n, 30, passes_v, n)
                 at(n + 1, 25, add_bias, n)
                 at(n + 2, 60, quant_vp, n)
-                if h == 1:
-                    at(n + 1, 63, mul, a)
-                    at(n + 2, 64, quant_attn, a)
-                    at(n + 3, 45, passes_o, a, n)
-                    at(n + 3, 50, finish, a)
+        late = 0
+        for n in range(N):
+            kind, a, h = seq[n]
+            if kind == "v" and h == 1:
+                step = max(n + 3, qa_step + 1 + late // 2)
+                late += 1
+                at(step, 45, passes_o, a)
+                at(step, 45, finish, a)
         at(W_STEP, 1, w_flip)
         at(W_STEP, 21, w_evac)
         at(W_STEP + 1, 11, w_quant)

@@ -16,20 +16,38 @@ B, L, D, DV, BN = 8, 1024, 1024, 256, 128
 P = 128
 FLOPS = 2 * B * L * D * DV + 2 * B * BN * L * D + 2 * B * BN * L * DV
 
-PINNED = False
-RAW_BUFS = 8
-AHEAD = 3
-RAMP = 0
-W_STEP = 8
-PE_SUM = True
-V_EVAC_HEAD = 3
-V_EVAC_TAIL = 0
-EXP_AT = [1,2,3,4]
-SUM_AT = 5
-RCP_AT = 6
-BACK_AT = 7
-MUL_AT = [8,8,9,9]
-QA_AT = 10
+RAW_BUFS = 7
+GRP = 4
+COD = 3
+AHEAD = 2
+QLEAD = 1
+W_AT = 8
+W_LOAD = 6
+WARM_0 = 8
+WARM_N = 1
+WARM_TO = 18
+VE_FIRST = 4
+VE_LAST = 9
+EXP_RATE = 2
+SUM_LAG = 1
+RCP_PIECES = 2
+MUL_RATE = 2
+QVP = 2
+XT = 4
+ACC = 3
+MSC = 1
+DD = 3
+EE = 2
+SPLIT = 2
+TAIL_VE = 1
+VE_MOD = 2
+RCP_S = 0
+RB_COPY = 1
+MLAG = 1
+HELP = ()
+VMIX = ()
+VF = 0
+VF2 = 0
 
 
 def tile_bottleneck_attention_pa_t_kernel(tc, qp_top, kp, v, Wv, bv, out):
@@ -37,17 +55,16 @@ def tile_bottleneck_attention_pa_t_kernel(tc, qp_top, kp, v, Wv, bv, out):
     with ExitStack() as ctx:
         const = ctx.enter_context(tc.tile_pool(name="const", bufs=1))
         rawp = ctx.enter_context(tc.tile_pool(name="rawp", bufs=RAW_BUFS))
-        grpp = ctx.enter_context(tc.tile_pool(name="grpp", bufs=3))
-        codp = ctx.enter_context(tc.tile_pool(name="codp", bufs=3))
-        dep = ctx.enter_context(tc.tile_pool(name="dep", bufs=3))
+        grpp = ctx.enter_context(tc.tile_pool(name="grpp", bufs=GRP))
+        codp = ctx.enter_context(tc.tile_pool(name="codp", bufs=COD))
+        dep = ctx.enter_context(tc.tile_pool(name="dep", bufs=DD))
         smp = ctx.enter_context(tc.tile_pool(name="smp", bufs=2))
         vpp = ctx.enter_context(tc.tile_pool(name="vpp", bufs=3))
-        otp = ctx.enter_context(tc.tile_pool(name="otp", bufs=4))
-        xtp = ctx.enter_context(tc.psum_pool(name="xtp", bufs=4))
-        accp = ctx.enter_context(tc.psum_pool(name="accp", bufs=3))
-        mscp = ctx.enter_context(tc.psum_pool(name="mscp", bufs=1))
-        if PINNED:
-            ctx.enter_context(tc.manual_schedule())
+        otp = ctx.enter_context(tc.tile_pool(name="otp", bufs=2))
+        xtp = ctx.enter_context(tc.psum_pool(name="xtp", bufs=XT))
+        accp = ctx.enter_context(tc.psum_pool(name="accp", bufs=ACC))
+        mscp = ctx.enter_context(tc.psum_pool(name="mscp", bufs=MSC))
+        ctx.enter_context(tc.manual_schedule())
 
         ident = const.tile([P, P], F32, name="ident")
         make_identity(nc, ident[:])
@@ -68,9 +85,16 @@ def tile_bottleneck_attention_pa_t_kernel(tc, qp_top, kp, v, Wv, bv, out):
         kview = kp.rearrange("b (g p t) d -> g t p b d", g=2, p=P, t=4)
         vview = v.rearrange("b (g p t) d -> b g p t d", g=2, p=P, t=4)
 
-        seq = [("q", 0, 0), ("k", 0, 0), ("q", 1, 0), ("k", 0, 1)]
-        seq.extend([("k", u, h) for u in range(1, 8) for h in range(2)])
-        seq.extend([("v", b, g) for b in range(B) for g in range(2)])
+        vs = [("v", b, g) for b in range(B) for g in range(2)]
+        seq = vs[:VF] + [("q", 0, 0), ("k", 0, 0)] + vs[VF:VF2] + [("q", 1, 0), ("k", 0, 1)]
+        vi = VF2
+        for u in range(1, 8):
+            for h in range(2):
+                seq.append(("k", u, h))
+                if 2 * u + h in VMIX:
+                    seq.append(vs[vi])
+                    vi += 1
+        seq.extend(vs[vi:])
         N = len(seq)
 
         raws, xts, grps, cods, scas, accs = {}, {}, {}, {}, {}, {}
@@ -85,11 +109,18 @@ def tile_bottleneck_attention_pa_t_kernel(tc, qp_top, kp, v, Wv, bv, out):
             else:
                 src = vview[a, h]
             raw = rawp.tile([P, 4096], BF16, name="raw", tag="raw")
-            nc.sync.dma_start(out=raw[:].rearrange("p (s d) -> p s d", s=4), in_=src)
+            dst = raw[:].rearrange("p (s d) -> p s d", s=4)
+            pieces = 4 if n < SPLIT else 1
+            w = 4 // pieces
+            for i in range(pieces):
+                nc.sync.dma_start(out=raw[:, 4096 // pieces * i : 4096 // pieces * (i + 1)].rearrange("p (s d) -> p s d", s=w),
+                                  in_=src[:, w * i : w * i + w, :])
             raws[n] = raw
 
-        def flip_slab(words, s):
+        def flip_slab(words, s, warm=0):
             xt = xtp.tile([P, 512], F32, name="xt", tag="xt")
+            for i in range(warm):
+                nc.tensor.matmul(out=xt[:, 0:P], lhsT=ident[:], rhs=ident[:], start=True, stop=True)
             for q in range(4):
                 lo = 512 * s + 128 * q
                 nc.tensor.transpose(xt[:, 128 * q : 128 * q + 128], words[:, lo : lo + 128], ident[:])
@@ -105,17 +136,30 @@ def tile_bottleneck_attention_pa_t_kernel(tc, qp_top, kp, v, Wv, bv, out):
 
         def flip(n):
             words = raws[n][:].bitcast(F32)
-            xts[n] = [flip_slab(words, s) for s in range(4)]
+            warm = WARM_0 if n == 0 else (WARM_N if n < WARM_TO else 0)
+            xts[n] = [flip_slab(words, s, warm if s == 0 else 0) for s in range(4)]
             if n + RAW_BUFS < N:
                 load(n + RAW_BUFS)
+
+        def vector_slabs(n):
+            if n >= N - TAIL_VE:
+                return (1, 3)
+            if VE_FIRST <= n < VE_LAST and n % VE_MOD == 1:
+                return (3,)
+            return ()
 
         def evac(n):
             grp = grpp.tile([P, 4096], BF16, name="grp", tag="grp", align_bytes=64)
             gf = grp[:].bitcast(F32)
             for s in range(4):
-                on_vector = (n < V_EVAC_HEAD or n >= N - V_EVAC_TAIL) and s >= 2
-                evac_slab(on_vector, gf, xts[n][s], s)
+                if s not in vector_slabs(n):
+                    evac_slab(False, gf, xts[n][s], s)
             grps[n] = grp
+
+        def evac_v(n):
+            gf = grps[n][:].bitcast(F32)
+            for s in vector_slabs(n):
+                evac_slab(True, gf, xts[n][s], s)
 
         def quant(n):
             kind, a, h = seq[n]
@@ -153,7 +197,6 @@ def tile_bottleneck_attention_pa_t_kernel(tc, qp_top, kp, v, Wv, bv, out):
             accs[("k", u, h)] = sc
 
         def passes_v(n):
-            kind, b, g = seq[n]
             for h in range(2):
                 vb = accp.tile([P, 512], F32, name="vb", tag="acc")
                 for t in range(4):
@@ -169,57 +212,84 @@ def tile_bottleneck_attention_pa_t_kernel(tc, qp_top, kp, v, Wv, bv, out):
                 axis=AX.X, op=ALU.max)
             sm[("mh", u, h)] = mh
 
+        def help_copy(u):
+            hc = smp.tile([P, 512], BF16, name="hc", tag="hc")
+            nc.scalar.copy(out=hc[:], in_=accs[("k", u, 0)][:])
+            sm[("hc", u)] = hc
+
+        def help_max(u):
+            m4 = smp.tile([P, 512], BF16, name="m4", tag="m4")
+            nc.vector.tensor_tensor(out=m4[:], in0=accs[("k", u, 1)][:], in1=sm[("hc", u)][:], op=ALU.max)
+            m2 = smp.tile([P, 256], BF16, name="m2", tag="m2")
+            nc.vector.tensor_tensor(out=m2[:], in0=m4[:, 0:256], in1=m4[:, 256:512], op=ALU.max)
+            m = smp.tile([P, P], F32, name="m", tag="m")
+            nc.vector.tensor_tensor(out=m[:], in0=m2[:, 0:128], in1=m2[:, 128:256], op=ALU.max)
+            sm[("m", u)] = m
+
         def comb(u):
             m = smp.tile([P, P], F32, name="m", tag="m")
             nc.vector.tensor_tensor(out=m[:], in0=sm[("mh", u, 0)][:], in1=sm[("mh", u, 1)][:], op=ALU.max)
             sm[("m", u)] = m
 
         def sub(u, h):
-            g, t = u // 4, u % 4
-            if ("d", g) not in sm:
-                dg = dep.tile([P, 4096], F32, name="dg", tag="de")
-                sm[("d", g)] = dg
-            lo = 1024 * t + 512 * h
+            if ("d", u // 2) not in sm:
+                sm[("d", u // 2)] = dep.tile([P, 2048], F32, name="dd", tag="dd")
+            lo = 1024 * (u % 2) + 512 * h
             nc.vector.tensor_tensor(
-                out=sm[("d", g)][:, lo : lo + 512].rearrange("p (b i) -> p b i", b=4),
+                out=sm[("d", u // 2)][:, lo : lo + 512].rearrange("p (b i) -> p b i", b=4),
                 in0=accs[("k", u, h)][:].rearrange("p (b i) -> p b i", b=4),
                 in1=sm[("m", u)][:].unsqueeze(1).to_broadcast([P, 4, P]),
                 op=ALU.subtract)
 
-        def expo(g, x):
+        def expo(w, x):
+            g = w // 2
             if ("e", g) not in sm:
-                eg = dep.tile([P, 4096], F32, name="eg", tag="de")
-                sm[("e", g)] = eg
+                sm[("e", g)] = dep.tile([P, 4096], F32, name="ee", tag="ee", bufs=EE)
+            lo = 2048 * (w % 2) + 512 * x
             nc.scalar.activation(
-                out=sm[("e", g)][:, 1024 * x : 1024 * x + 1024].rearrange("p (b i t) -> p b i t", b=2, i=P, t=4),
-                in_=sm[("d", g)][:].rearrange("p (t b i) -> p b i t", t=4, b=B, i=P)[:, 2 * x : 2 * x + 2],
+                out=sm[("e", g)][:, lo : lo + 512].rearrange("p (c t) -> p c t", t=2),
+                in_=sm[("d", w)][:].rearrange("p (t c) -> p c t", t=2)[:, 256 * x : 256 * x + 256, :],
                 func=ACT.Exp, scale=1.0 / 32.0)
 
-        def sum_pe(g):
-            sb = mscp.tile([P, 512], F32, name="sb", tag="msc")
+        def sum_pe(w, k):
+            g = w // 2
+            if ("sb", g) not in sm:
+                sm[("sb", g)] = mscp.tile([P, 512], F32, name="sb", tag="msc")
+            sb = sm[("sb", g)]
             eg = sm[("e", g)]
-            for k in range(4):
-                for b in range(B):
-                    nc.tensor.matmul(out=sb[:, P * k : P * k + P], lhsT=eg[:, 512 * b + P * k : 512 * b + P * k + P],
-                                     rhs=ident[:], is_transpose=True, start=(b == 0), stop=(b == B - 1))
-            sm[("sb", g)] = sb
+            o = 256 * (w % 2) + P * k
+            for b in range(B):
+                lo = 2048 * (w % 2) + 256 * b + P * k
+                nc.tensor.matmul(out=sb[:, o : o + P], lhsT=eg[:, lo : lo + P],
+                                 rhs=ident[:], is_transpose=True, start=(b == 0), stop=(b == B - 1))
 
-        def recip(g):
-            rt = smp.tile([P, 512], F32, name="rt", tag="rt")
-            nc.vector.reciprocal(out=rt[:], in_=sm[("sb", g)][:])
-            sm[("rt", g)] = rt
+        def recip(g, x):
+            if ("rt", g) not in sm:
+                sm[("rt", g)] = smp.tile([P, 512], F32, name="rt", tag="rt")
+            wd = 512 // RCP_PIECES
+            nc.vector.reciprocal(out=sm[("rt", g)][:, wd * x : wd * x + wd], in_=sm[("sb", g)][:, wd * x : wd * x + wd])
+
+        def recip_s(g):
+            lt = smp.tile([P, 512], F32, name="lt", tag="lt")
+            nc.scalar.activation(out=lt[:], in_=sm[("sb", g)][:], func=ACT.Ln)
+            sm[("rt", g)] = smp.tile([P, 512], F32, name="rt", tag="rt")
+            nc.scalar.activation(out=sm[("rt", g)][:], in_=lt[:], func=ACT.Exp, scale=-1.0)
 
         def back_pe(g):
             rb = mscp.tile([P, 512], F32, name="rb", tag="msc")
             for k in range(4):
                 nc.tensor.transpose(rb[:, P * k : P * k + P], sm[("rt", g)][:, P * k : P * k + P], ident[:])
+            if RB_COPY:
+                rs = smp.tile([P, 512], F32, name="rs", tag="rs", bufs=1)
+                nc.scalar.copy(out=rs[:], in_=rb[:])
+                rb = rs
             sm[("rb", g)] = rb
 
-        def mul(g, x):
+        def mul(g, b):
             nc.vector.tensor_tensor(
-                out=ag[:, 1024 * x : 1024 * x + 1024].rearrange("p (b c) -> p b c", b=2),
-                in0=sm[("e", g)][:, 1024 * x : 1024 * x + 1024].rearrange("p (b c) -> p b c", b=2),
-                in1=sm[("rb", g)][:].unsqueeze(1).to_broadcast([P, 2, 512]),
+                out=ag[:, 512 * b : 512 * b + 512].rearrange("p (i w t) -> p i w t", w=2, t=2),
+                in0=sm[("e", g)][:].rearrange("p (w b i t) -> p b i w t", w=2, b=B, t=2)[:, b],
+                in1=sm[("rb", g)][:].rearrange("p (w i t) -> p i w t", w=2, t=2),
                 op=ALU.mult)
 
         def quant_attn(g):
@@ -243,15 +313,19 @@ def tile_bottleneck_attention_pa_t_kernel(tc, qp_top, kp, v, Wv, bv, out):
                                   in_=sm[("vg", n)][:])
 
         def passes_o(b):
-            ob = mscp.tile([P, 512], F32, name="ob", tag="msc")
-            for g in range(2):
-                mx(ob[:, 0:DV], acod, asca, 1024 * g + P * b, pcod, psca, 256 * (2 * b + g), DV, g)
+            ob = xtp.tile([P, 512], F32, name="ob", tag="xt")
+            for j in range(2):
+                for g in range(2):
+                    mx(ob[:, DV * j : DV * j + DV], acod, asca, 1024 * g + P * (b + j), pcod, psca, 256 * (2 * (b + j) + g), DV, g)
             accs[("o", b)] = ob
 
         def finish(b):
-            ot = otp.tile([P, DV], F32, name="ot", tag="ot")
-            nc.scalar.copy(out=ot[:], in_=accs[("o", b)][:, 0:DV])
-            nc.sync.dma_start(out=out[b], in_=ot[:])
+            ot = otp.tile([P, 512], F32, name="ot", tag="ot")
+            if b % 4 == 2:
+                nc.vector.tensor_copy(out=ot[:], in_=accs[("o", b)][:])
+            else:
+                nc.scalar.copy(out=ot[:], in_=accs[("o", b)][:])
+            nc.sync.dma_start(out=out[b : b + 2].rearrange("b i n -> i b n"), in_=ot[:].rearrange("p (b n) -> p b n", b=2))
 
         def w_flip():
             words = wraw[:].bitcast(F32)
@@ -265,58 +339,112 @@ def tile_bottleneck_attention_pa_t_kernel(tc, qp_top, kp, v, Wv, bv, out):
         def w_quant():
             nc.vector.quantize_mx(out=wcod[:].bitcast(FP8X4), scales=wsca[:], in_=wgrp[:])
 
-        plan = {}
-
-        def at(step, slot, fn, *args):
-            plan[(step, slot)] = plan.get((step, slot), []) + [(fn, args)]
-
-        qa_step = 0
-        for n in range(N):
-            kind, a, h = seq[n]
-            ahead = min(AHEAD, 1 + n // RAMP) if RAMP else AHEAD
-            at(n - ahead, 0, flip, n)
-            at(n - ahead, 20, evac, n)
-            at(n, 10, quant, n)
-            if kind == "k":
-                at(n, 30, passes_k, n)
-                if h == 1:
-                    at(n, 61, half_max, a, 0)
-                    at(n + 1, 40, half_max, a, 1)
-                    at(n + 1, 42, comb, a)
-                    at(n + 1, 44, sub, a, 0)
-                    at(n + 1, 44, sub, a, 1)
-                    if a % 4 == 3:
-                        g = a // 4
-                        for x in range(4):
-                            at(n + EXP_AT[x], 50, expo, g, x)
-                            at(n + MUL_AT[x], 63, mul, g, x)
-                        at(n + SUM_AT, 2, sum_pe, g)
-                        at(n + RCP_AT, 12, recip, g)
-                        at(n + BACK_AT, 2, back_pe, g)
-                        at(n + QA_AT, 64, quant_attn, g)
-                        qa_step = n + QA_AT
-            if kind == "v":
-                at(n, 30, passes_v, n)
-                at(n + 1, 25, add_bias, n)
-                at(n + 2, 60, quant_vp, n)
-        late = 0
-        for n in range(N):
-            kind, a, h = seq[n]
-            if kind == "v" and h == 1:
-                step = max(n + 3, qa_step + 1 + late // 2)
-                late += 1
-                at(step, 45, passes_o, a)
-                at(step, 45, finish, a)
-        at(W_STEP, 1, w_flip)
-        at(W_STEP, 21, w_evac)
-        at(W_STEP + 1, 11, w_quant)
-
-        for n in range(min(RAW_BUFS, N)):
-            load(n)
-            if n == 3:
+        for n in range(-1, RAW_BUFS):
+            if n >= 0:
+                load(n)
+            if n == W_LOAD:
                 nc.sync.dma_start(out=wraw[:].rearrange("p (h d) -> p h d", h=2),
                                   in_=Wv.rearrange("(h p) d -> p h d", p=P))
                 nc.sync.dma_start(out=bias[:], in_=bv.partition_broadcast(P))
-        for key in sorted(plan):
-            for fn, args in plan[key]:
-                fn(*args)
+
+        exps, peq, vq = [], [], []
+        ready_o = []
+        attn_done = False
+        vdone = set()
+        n = -AHEAD
+        waits = {}
+        free_from = 0
+        while n < N + 4 or exps or peq or vq or ready_o:
+            m = n - 1
+            if 0 <= n + AHEAD < N:
+                flip(n + AHEAD)
+                evac(n + AHEAD)
+            if n + AHEAD == W_AT:
+                w_flip()
+                w_evac()
+            for f in waits.pop(("pe", n), []):
+                f()
+            if 0 <= m < N:
+                kind, a, h = seq[m]
+                if kind == "k":
+                    if a in HELP:
+                        if h == 0:
+                            help_copy(a)
+                        else:
+                            help_max(a)
+                    else:
+                        half_max(a, h)
+                        if h == 1:
+                            comb(a)
+                    if h == 1:
+                        sub(a, 0)
+                        sub(a, 1)
+                        if a % 2 == 1:
+                            w = a // 2
+                            exps.extend([(w, x) for x in range(4)])
+                if kind == "v":
+                    add_bias(m)
+            if n + AHEAD == W_AT + 1:
+                w_quant()
+            if 0 <= n + QLEAD < N:
+                quant(n + QLEAD)
+            if 0 <= n + AHEAD < N:
+                evac_v(n + AHEAD)
+            for f in waits.pop(("v", n), []):
+                f()
+            if vq:
+                for f in vq.pop(0):
+                    f()
+            for f in waits.pop(("s", n), []):
+                f()
+            for i in range(EXP_RATE):
+                if exps:
+                    w, x = exps.pop(0)
+                    expo(w, x)
+                    if x == 3:
+                        s = max(n + SUM_LAG, free_from)
+                        for k in range(2):
+                            waits.setdefault(("pe", s + k), []).append(lambda w=w, k=k: sum_pe(w, k))
+                        free_from = s + 2
+                        if w % 2 == 1:
+                            g = w // 2
+                            s = s + 2
+                            if RCP_S:
+                                waits.setdefault(("s", s), []).append(lambda g=g: recip_s(g))
+                                s = s + 1
+                            else:
+                                for r in range(RCP_PIECES):
+                                    waits.setdefault(("v", s + r), []).append(lambda g=g, r=r: recip(g, r))
+                                s = s + RCP_PIECES + 1
+                            waits.setdefault(("pe", s), []).append(lambda g=g: back_pe(g))
+                            for b in range(B):
+                                waits.setdefault(("v", s + 1 + b // MUL_RATE), []).append(lambda g=g, b=b: mul(g, b))
+                            if RB_COPY:
+                                free_from = s + 1
+                            s = s + 1 + B // MUL_RATE
+                            waits.setdefault(("v", s), []).append(lambda g=g: quant_attn(g))
+                            if not RB_COPY:
+                                free_from = s
+                            if g == 1:
+                                waits.setdefault(("o", s + 1), []).append(None)
+            mm = n - QVP
+            if 0 <= mm < N and seq[mm][0] == "v":
+                quant_vp(mm)
+                kind, b, g = seq[mm]
+                vdone.add((b, g))
+                if all((2 * (b // 2) + j, y) in vdone for j in range(2) for y in range(2)):
+                    ready_o.append(2 * (b // 2))
+            if 0 <= n < N:
+                if seq[n][0] == "k":
+                    passes_k(n)
+                if seq[n][0] == "v":
+                    passes_v(n)
+            if waits.pop(("o", n), []):
+                attn_done = True
+            if attn_done:
+                for i in range(2):
+                    if ready_o:
+                        b = ready_o.pop(0)
+                        passes_o(b)
+                        finish(b)
+            n += 1

@@ -16,22 +16,25 @@ B, L, D, DV, BN = 8, 1024, 1024, 256, 128
 P = 128
 FLOPS = 2 * B * L * D * DV + 2 * B * BN * L * D + 2 * B * BN * L * DV
 
-RAW_BUFS = 7
+RAW_BUFS = 6
 GRP = 4
 COD = 3
 AHEAD = 2
 QLEAD = 1
 W_AT = 8
-W_LOAD = 6
+W_LOAD = 5
 WARM_0 = 8
 WARM_N = 1
-WARM_TO = 18
+WARM_TO = 8
 VE_FIRST = 4
-VE_LAST = 9
+VE_LAST = 13
 EXP_RATE = 2
 SUM_LAG = 1
 RCP_PIECES = 2
 MUL_RATE = 2
+MULB = 2
+EXPW = 2
+QPAIR = 1
 QVP = 2
 XT = 4
 ACC = 3
@@ -40,8 +43,9 @@ DD = 3
 EE = 2
 SPLIT = 2
 TAIL_VE = 1
-VE_MOD = 2
-RCP_S = 0
+VE_MOD = 1
+RCP_S = (0, 1)
+RCP_SPLIT = 1
 RB_COPY = 1
 MLAG = 1
 HELP = ()
@@ -59,7 +63,7 @@ def tile_bottleneck_attention_pa_t_kernel(tc, qp_top, kp, v, Wv, bv, out):
         codp = ctx.enter_context(tc.tile_pool(name="codp", bufs=COD))
         dep = ctx.enter_context(tc.tile_pool(name="dep", bufs=DD))
         smp = ctx.enter_context(tc.tile_pool(name="smp", bufs=2))
-        vpp = ctx.enter_context(tc.tile_pool(name="vpp", bufs=3))
+        vpp = ctx.enter_context(tc.tile_pool(name="vpp", bufs=2))
         otp = ctx.enter_context(tc.tile_pool(name="otp", bufs=2))
         xtp = ctx.enter_context(tc.psum_pool(name="xtp", bufs=XT))
         accp = ctx.enter_context(tc.psum_pool(name="accp", bufs=ACC))
@@ -144,7 +148,7 @@ def tile_bottleneck_attention_pa_t_kernel(tc, qp_top, kp, v, Wv, bv, out):
         def vector_slabs(n):
             if n >= N - TAIL_VE:
                 return (1, 3)
-            if VE_FIRST <= n < VE_LAST and n % VE_MOD == 1:
+            if VE_FIRST <= n < VE_LAST and n % VE_MOD == VE_MOD - 1:
                 return (3,)
             return ()
 
@@ -247,8 +251,8 @@ def tile_bottleneck_attention_pa_t_kernel(tc, qp_top, kp, v, Wv, bv, out):
                 sm[("e", g)] = dep.tile([P, 4096], F32, name="ee", tag="ee", bufs=EE)
             lo = 2048 * (w % 2) + 512 * x
             nc.scalar.activation(
-                out=sm[("e", g)][:, lo : lo + 512].rearrange("p (c t) -> p c t", t=2),
-                in_=sm[("d", w)][:].rearrange("p (t c) -> p c t", t=2)[:, 256 * x : 256 * x + 256, :],
+                out=sm[("e", g)][:, lo : lo + 512 * EXPW].rearrange("p (c t) -> p c t", t=2),
+                in_=sm[("d", w)][:].rearrange("p (t c) -> p c t", t=2)[:, 256 * x : 256 * x + 256 * EXPW, :],
                 func=ACT.Exp, scale=1.0 / 32.0)
 
         def sum_pe(w, k):
@@ -269,9 +273,12 @@ def tile_bottleneck_attention_pa_t_kernel(tc, qp_top, kp, v, Wv, bv, out):
             wd = 512 // RCP_PIECES
             nc.vector.reciprocal(out=sm[("rt", g)][:, wd * x : wd * x + wd], in_=sm[("sb", g)][:, wd * x : wd * x + wd])
 
-        def recip_s(g):
-            lt = smp.tile([P, 512], F32, name="lt", tag="lt")
-            nc.scalar.activation(out=lt[:], in_=sm[("sb", g)][:], func=ACT.Ln)
+        def recip_ln(g):
+            sm[("lt", g)] = smp.tile([P, 512], F32, name="lt", tag="lt", bufs=1)
+            nc.scalar.activation(out=sm[("lt", g)][:], in_=sm[("sb", g)][:], func=ACT.Ln)
+
+        def recip_exp(g):
+            lt = sm[("lt", g)]
             sm[("rt", g)] = smp.tile([P, 512], F32, name="rt", tag="rt")
             nc.scalar.activation(out=sm[("rt", g)][:], in_=lt[:], func=ACT.Exp, scale=-1.0)
 
@@ -281,15 +288,16 @@ def tile_bottleneck_attention_pa_t_kernel(tc, qp_top, kp, v, Wv, bv, out):
                 nc.tensor.transpose(rb[:, P * k : P * k + P], sm[("rt", g)][:, P * k : P * k + P], ident[:])
             if RB_COPY:
                 rs = smp.tile([P, 512], F32, name="rs", tag="rs", bufs=1)
-                nc.scalar.copy(out=rs[:], in_=rb[:])
+                nc.scalar.copy(out=rs[:].rearrange("p (i w t) -> p i w t", w=2, t=2),
+                               in_=rb[:].rearrange("p (w i t) -> p i w t", w=2, t=2))
                 rb = rs
             sm[("rb", g)] = rb
 
         def mul(g, b):
             nc.vector.tensor_tensor(
-                out=ag[:, 512 * b : 512 * b + 512].rearrange("p (i w t) -> p i w t", w=2, t=2),
-                in0=sm[("e", g)][:].rearrange("p (w b i t) -> p b i w t", w=2, b=B, t=2)[:, b],
-                in1=sm[("rb", g)][:].rearrange("p (w i t) -> p i w t", w=2, t=2),
+                out=ag[:, 512 * b : 512 * (b + MULB)].rearrange("p (b i w t) -> p b i w t", b=MULB, w=2, t=2),
+                in0=sm[("e", g)][:].rearrange("p (w b i t) -> p b i w t", w=2, b=B, t=2)[:, b : b + MULB],
+                in1=sm[("rb", g)][:].rearrange("p (i w t) -> p i w t", w=2, t=2).unsqueeze(1).to_broadcast([P, MULB, P, 2, 2]),
                 op=ALU.mult)
 
         def quant_attn(g):
@@ -297,20 +305,24 @@ def tile_bottleneck_attention_pa_t_kernel(tc, qp_top, kp, v, Wv, bv, out):
                                   scales=asca[:, 1024 * g : 1024 * g + 1024], in_=ag[:])
 
         def add_bias(n):
-            vg = vpp.tile([P, 1024], BF16, name="vg", tag="vg", align_bytes=64)
+            kind, b, g = seq[n]
+            if g == 0:
+                sm[("vg", b)] = vpp.tile([P, 2048], BF16, name="vg", tag="vg", align_bytes=64)
+            vg = sm[("vg", b)]
             for h in range(2):
+                lo = 1024 * g + 512 * h
                 nc.vector.tensor_tensor(
-                    out=vg[:, 512 * h : 512 * h + 512].rearrange("p (n t) -> p n t", t=4),
+                    out=vg[:, lo : lo + 512].rearrange("p (n t) -> p n t", t=4),
                     in0=accs[("v", n, h)][:].rearrange("p (t n) -> p n t", t=4),
                     in1=bias[:, P * h : P * h + P].unsqueeze(2).to_broadcast([P, P, 4]),
                     op=ALU.add)
-            sm[("vg", n)] = vg
 
         def quant_vp(n):
             kind, b, g = seq[n]
-            lo = 256 * (2 * b + g)
-            nc.vector.quantize_mx(out=pcod[:, lo : lo + 256].bitcast(FP8X4), scales=psca[:, lo : lo + 256],
-                                  in_=sm[("vg", n)][:])
+            if g == 1:
+                lo = 512 * b
+                nc.vector.quantize_mx(out=pcod[:, lo : lo + 512].bitcast(FP8X4), scales=psca[:, lo : lo + 512],
+                                      in_=sm[("vg", b)][:])
 
         def passes_o(b):
             ob = xtp.tile([P, 512], F32, name="ob", tag="xt")
@@ -381,7 +393,7 @@ def tile_bottleneck_attention_pa_t_kernel(tc, qp_top, kp, v, Wv, bv, out):
                         sub(a, 1)
                         if a % 2 == 1:
                             w = a // 2
-                            exps.extend([(w, x) for x in range(4)])
+                            exps.extend([(w, x) for x in range(0, 4, EXPW)])
                 if kind == "v":
                     add_bias(m)
             if n + AHEAD == W_AT + 1:
@@ -397,11 +409,11 @@ def tile_bottleneck_attention_pa_t_kernel(tc, qp_top, kp, v, Wv, bv, out):
                     f()
             for f in waits.pop(("s", n), []):
                 f()
-            for i in range(EXP_RATE):
+            for i in range(EXP_RATE // EXPW):
                 if exps:
                     w, x = exps.pop(0)
                     expo(w, x)
-                    if x == 3:
+                    if x == 4 - EXPW:
                         s = max(n + SUM_LAG, free_from)
                         for k in range(2):
                             waits.setdefault(("pe", s + k), []).append(lambda w=w, k=k: sum_pe(w, k))
@@ -409,15 +421,16 @@ def tile_bottleneck_attention_pa_t_kernel(tc, qp_top, kp, v, Wv, bv, out):
                         if w % 2 == 1:
                             g = w // 2
                             s = s + 2
-                            if RCP_S:
-                                waits.setdefault(("s", s), []).append(lambda g=g: recip_s(g))
-                                s = s + 1
+                            if RCP_S[g]:
+                                waits.setdefault(("s", s), []).append(lambda g=g: recip_ln(g))
+                                waits.setdefault(("s", s + RCP_SPLIT), []).append(lambda g=g: recip_exp(g))
+                                s = s + 1 + RCP_SPLIT
                             else:
                                 for r in range(RCP_PIECES):
                                     waits.setdefault(("v", s + r), []).append(lambda g=g, r=r: recip(g, r))
                                 s = s + RCP_PIECES + 1
                             waits.setdefault(("pe", s), []).append(lambda g=g: back_pe(g))
-                            for b in range(B):
+                            for b in range(0, B, MULB):
                                 waits.setdefault(("v", s + 1 + b // MUL_RATE), []).append(lambda g=g, b=b: mul(g, b))
                             if RB_COPY:
                                 free_from = s + 1

@@ -17,7 +17,7 @@ P = 128
 FLOPS = 2 * B * L * D * DV + 2 * B * BN * L * D + 2 * B * BN * L * DV
 
 RAW_BUFS = 6
-GRP = 4
+GRP = 3
 COD = 3
 AHEAD = 2
 QLEAD = 1
@@ -25,9 +25,9 @@ W_AT = 8
 W_LOAD = 5
 WARM_0 = 8
 WARM_N = 1
-WARM_TO = 8
+WARM_TO = 12
 VE_FIRST = 4
-VE_LAST = 13
+VE_LAST = 0
 EXP_RATE = 2
 SUM_LAG = 1
 RCP_PIECES = 2
@@ -36,13 +36,16 @@ MULB = 2
 EXPW = 2
 QPAIR = 1
 QVP = 2
+BGRP = ((1, 1), (3, 1), (5, 1))
+TVE = 0
+OUT_V = 0
 XT = 4
 ACC = 3
 MSC = 1
 DD = 3
 EE = 2
 SPLIT = 2
-TAIL_VE = 1
+TAIL_VE = 0
 VE_MOD = 1
 RCP_S = (0, 1)
 RCP_SPLIT = 1
@@ -63,7 +66,7 @@ def tile_bottleneck_attention_pa_t_kernel(tc, qp_top, kp, v, Wv, bv, out):
         codp = ctx.enter_context(tc.tile_pool(name="codp", bufs=COD))
         dep = ctx.enter_context(tc.tile_pool(name="dep", bufs=DD))
         smp = ctx.enter_context(tc.tile_pool(name="smp", bufs=2))
-        vpp = ctx.enter_context(tc.tile_pool(name="vpp", bufs=2))
+        vpp = ctx.enter_context(tc.tile_pool(name="vpp", bufs=3))
         otp = ctx.enter_context(tc.tile_pool(name="otp", bufs=2))
         xtp = ctx.enter_context(tc.psum_pool(name="xtp", bufs=XT))
         accp = ctx.enter_context(tc.psum_pool(name="accp", bufs=ACC))
@@ -79,6 +82,8 @@ def tile_bottleneck_attention_pa_t_kernel(tc, qp_top, kp, v, Wv, bv, out):
         wcod = const.tile([P, 512], U32, name="wcod", align_bytes=64)
         wsca = const.tile([P, 512], U8, name="wsca", align_bytes=64)
         bias = const.tile([P, DV], BF16, name="bias")
+        biasf = const.tile([P, DV], F32, name="biasf")
+        bcol = const.tile([P, 2], F32, name="bcol")
         pcod = const.tile([P, 4096], U32, name="pcod", align_bytes=64)
         psca = const.tile([P, 4096], U8, name="psca", align_bytes=64)
         acod = const.tile([P, 2048], U32, name="acod", align_bytes=64)
@@ -130,8 +135,11 @@ def tile_bottleneck_attention_pa_t_kernel(tc, qp_top, kp, v, Wv, bv, out):
                 nc.tensor.transpose(xt[:, 128 * q : 128 * q + 128], words[:, lo : lo + 128], ident[:])
             return xt
 
-        def evac_slab(eng_is_vector, gf, xt, s):
-            dst = gf[:, 512 * s : 512 * s + 512].rearrange("p (c r u) -> p c r u", c=2, r=P, u=2)
+        def evac_slab(eng_is_vector, gf, xt, s, wide=False):
+            if wide:
+                dst = gf.rearrange("p (c t r u) -> p t c r u", c=2, t=4, r=P, u=2)[:, s]
+            else:
+                dst = gf[:, 512 * s : 512 * s + 512].rearrange("p (c r u) -> p c r u", c=2, r=P, u=2)
             src = xt[:].rearrange("p (c u r) -> p c r u", c=2, u=2, r=P)
             if eng_is_vector:
                 nc.vector.tensor_copy(out=dst, in_=src)
@@ -145,6 +153,9 @@ def tile_bottleneck_attention_pa_t_kernel(tc, qp_top, kp, v, Wv, bv, out):
             if n + RAW_BUFS < N:
                 load(n + RAW_BUFS)
 
+        def is_b(n):
+            return 0 <= n < N and seq[n][0] == "v" and (seq[n][1], seq[n][2]) in BGRP
+
         def vector_slabs(n):
             if n >= N - TAIL_VE:
                 return (1, 3)
@@ -157,13 +168,13 @@ def tile_bottleneck_attention_pa_t_kernel(tc, qp_top, kp, v, Wv, bv, out):
             gf = grp[:].bitcast(F32)
             for s in range(4):
                 if s not in vector_slabs(n):
-                    evac_slab(False, gf, xts[n][s], s)
+                    evac_slab(False, gf, xts[n][s], s, is_b(n))
             grps[n] = grp
 
         def evac_v(n):
             gf = grps[n][:].bitcast(F32)
             for s in vector_slabs(n):
-                evac_slab(True, gf, xts[n][s], s)
+                evac_slab(True, gf, xts[n][s], s, is_b(n))
 
         def quant(n):
             kind, a, h = seq[n]
@@ -208,6 +219,42 @@ def tile_bottleneck_attention_pa_t_kernel(tc, qp_top, kp, v, Wv, bv, out):
                         mx(vb[:, P * t : P * t + P], cods[n], scas[n], (2 * t + c) * P,
                            wcod, wsca, (2 * h + c) * P, P, c)
                 accs[("v", n, h)] = vb
+
+        def passes_w(n):
+            for h in range(2):
+                vb = accp.tile([P, 512], F32, name="vb", tag="acc")
+                for c in range(2):
+                    mx(vb[:], wcod, wsca, (2 * h + c) * P, cods[n], scas[n], 512 * c, 512, c)
+                accs[("v", n, h)] = vb
+
+        def bias_s(n):
+            vt = vpp.tile([P, 1024], BF16, name="vt", tag="vt", bufs=2)
+            for h in range(2):
+                nc.scalar.activation(
+                    out=vt[:, 512 * h : 512 * h + 512].rearrange("p (a r t) -> p a r t", a=2, r=P, t=2),
+                    in_=accs[("v", n, h)][:].rearrange("p (a t r) -> p a r t", a=2, t=2, r=P),
+                    func=ACT.Identity, bias=bcol[:, h : h + 1])
+            sm[("vt", n)] = vt
+
+        def flip_vt(n):
+            tv = accp.tile([P, 512], F32, name="tv", tag="acc")
+            words = sm[("vt", n)][:].bitcast(F32)
+            for q in range(4):
+                nc.tensor.transpose(tv[:, P * q : P * q + P], words[:, P * q : P * q + P], ident[:])
+            sm[("tv", n)] = tv
+
+        def evac_vt(n):
+            kind, b, g = seq[n]
+            if ("vg", b) not in sm:
+                sm[("vg", b)] = vpp.tile([P, 2048], BF16, name="vg", tag="vg", align_bytes=64)
+            evac_slab(TVE, sm[("vg", b)][:, 1024 * g : 1024 * g + 1024].bitcast(F32), sm[("tv", n)], 0)
+
+        def bias_columns():
+            nc.vector.tensor_copy(out=biasf[:], in_=bias[:])
+            xb = xtp.tile([P, 512], F32, name="xb", tag="xt")
+            for h in range(2):
+                nc.tensor.transpose(xb[:, P * h : P * h + P], biasf[:, P * h : P * h + P], ident[:])
+            nc.scalar.copy(out=bcol[:], in_=xb[:, 0 : 2 * P].rearrange("p (h x) -> p h x", h=2)[:, :, 0])
 
         def half_max(u, h):
             mh = smp.tile([P, P], F32, name="mh%d" % h, tag="mh%d" % h)
@@ -306,7 +353,7 @@ def tile_bottleneck_attention_pa_t_kernel(tc, qp_top, kp, v, Wv, bv, out):
 
         def add_bias(n):
             kind, b, g = seq[n]
-            if g == 0:
+            if ("vg", b) not in sm:
                 sm[("vg", b)] = vpp.tile([P, 2048], BF16, name="vg", tag="vg", align_bytes=64)
             vg = sm[("vg", b)]
             for h in range(2):
@@ -319,10 +366,9 @@ def tile_bottleneck_attention_pa_t_kernel(tc, qp_top, kp, v, Wv, bv, out):
 
         def quant_vp(n):
             kind, b, g = seq[n]
-            if g == 1:
-                lo = 512 * b
-                nc.vector.quantize_mx(out=pcod[:, lo : lo + 512].bitcast(FP8X4), scales=psca[:, lo : lo + 512],
-                                      in_=sm[("vg", b)][:])
+            lo = 512 * b
+            nc.vector.quantize_mx(out=pcod[:, lo : lo + 512].bitcast(FP8X4), scales=psca[:, lo : lo + 512],
+                                  in_=sm[("vg", b)][:])
 
         def passes_o(b):
             ob = xtp.tile([P, 512], F32, name="ob", tag="xt")
@@ -333,7 +379,7 @@ def tile_bottleneck_attention_pa_t_kernel(tc, qp_top, kp, v, Wv, bv, out):
 
         def finish(b):
             ot = otp.tile([P, 512], F32, name="ot", tag="ot")
-            if b % 4 == 2:
+            if b % 4 == 2 and OUT_V:
                 nc.vector.tensor_copy(out=ot[:], in_=accs[("o", b)][:])
             else:
                 nc.scalar.copy(out=ot[:], in_=accs[("o", b)][:])
@@ -368,12 +414,18 @@ def tile_bottleneck_attention_pa_t_kernel(tc, qp_top, kp, v, Wv, bv, out):
         free_from = 0
         while n < N + 4 or exps or peq or vq or ready_o:
             m = n - 1
+            if is_b(m):
+                bias_s(m)
             if 0 <= n + AHEAD < N:
                 flip(n + AHEAD)
                 evac(n + AHEAD)
+            if is_b(n - 2):
+                flip_vt(n - 2)
+                evac_vt(n - 2)
             if n + AHEAD == W_AT:
                 w_flip()
                 w_evac()
+                bias_columns()
             for f in waits.pop(("pe", n), []):
                 f()
             if 0 <= m < N:
@@ -394,7 +446,7 @@ def tile_bottleneck_attention_pa_t_kernel(tc, qp_top, kp, v, Wv, bv, out):
                         if a % 2 == 1:
                             w = a // 2
                             exps.extend([(w, x) for x in range(0, 4, EXPW)])
-                if kind == "v":
+                if kind == "v" and not is_b(m):
                     add_bias(m)
             if n + AHEAD == W_AT + 1:
                 w_quant()
@@ -440,18 +492,23 @@ def tile_bottleneck_attention_pa_t_kernel(tc, qp_top, kp, v, Wv, bv, out):
                                 free_from = s
                             if g == 1:
                                 waits.setdefault(("o", s + 1), []).append(None)
-            mm = n - QVP
-            if 0 <= mm < N and seq[mm][0] == "v":
-                quant_vp(mm)
+            for mm in (n - 3, n - 2):
+                if not (0 <= mm < N and seq[mm][0] == "v" and is_b(mm) == (mm == n - 3)):
+                    continue
                 kind, b, g = seq[mm]
                 vdone.add((b, g))
+                if (b, 1 - g) in vdone:
+                    quant_vp(mm)
                 if all((2 * (b // 2) + j, y) in vdone for j in range(2) for y in range(2)):
                     ready_o.append(2 * (b // 2))
             if 0 <= n < N:
                 if seq[n][0] == "k":
                     passes_k(n)
                 if seq[n][0] == "v":
-                    passes_v(n)
+                    if is_b(n):
+                        passes_w(n)
+                    else:
+                        passes_v(n)
             if waits.pop(("o", n), []):
                 attn_done = True
             if attn_done:

@@ -21,24 +21,29 @@ GRP = 3
 COD = 3
 AHEAD = 2
 QLEAD = 1
-W_AT = 8
+W_AT = 10
 W_LOAD = 5
 WARM_0 = 8
 WARM_N = 1
-WARM_TO = 12
+WARM_TO = 6
 VE_FIRST = 4
-VE_LAST = 0
+VE_LAST = 10
 EXP_RATE = 2
 SUM_LAG = 1
-RCP_PIECES = 2
+RCP_PIECES = 1
 MUL_RATE = 2
 MULB = 2
+EXP_DELAY = 1
+GPM = ()
+QA_LAG = (0, 0)
 EXPW = 2
 QPAIR = 1
 QVP = 2
-BGRP = ((1, 1), (3, 1), (5, 1))
+QSPLIT = 1
+BGRP = ((1, 1), (2, 1), (3, 1), (4, 1), (5, 1))
 TVE = 0
-OUT_V = 0
+LASTQ = 1
+LASTO = 1
 XT = 4
 ACC = 3
 MSC = 1
@@ -47,7 +52,7 @@ EE = 2
 SPLIT = 2
 TAIL_VE = 0
 VE_MOD = 1
-RCP_S = (0, 1)
+RCP_S = (0, 0)
 RCP_SPLIT = 1
 RB_COPY = 1
 MLAG = 1
@@ -176,19 +181,23 @@ def tile_bottleneck_attention_pa_t_kernel(tc, qp_top, kp, v, Wv, bv, out):
             for s in vector_slabs(n):
                 evac_slab(True, gf, xts[n][s], s, is_b(n))
 
-        def quant(n):
+        def quant(n, part=None):
             kind, a, h = seq[n]
             if kind == "q":
                 cod = qcod[:, 1024 * a : 1024 * a + 1024]
                 sca = qsca[:, 1024 * a : 1024 * a + 1024]
-            else:
+            elif part != 1:
                 codt = codp.tile([P, 1024], U32, name="codt", tag="codt", align_bytes=64)
                 scat = codp.tile([P, 1024], U8, name="scat", tag="scat", align_bytes=64)
                 cod = codt[:]
                 sca = scat[:]
-            nc.vector.quantize_mx(out=cod.bitcast(FP8X4), scales=sca, in_=grps[n][:])
+            else:
+                cod = cods[n]
+                sca = scas[n]
             cods[n] = cod
             scas[n] = sca
+            lo, hi = (0, 1024) if part is None else (512 * part, 512 * part + 512)
+            nc.vector.quantize_mx(out=cod[:, lo:hi].bitcast(FP8X4), scales=sca[:, lo:hi], in_=grps[n][:, 4 * lo : 4 * hi])
 
         def mx(acc, lc, ls, lo, rc, rs, ro, width, c):
             nc.tensor.matmul_mx(
@@ -364,26 +373,24 @@ def tile_bottleneck_attention_pa_t_kernel(tc, qp_top, kp, v, Wv, bv, out):
                     in1=bias[:, P * h : P * h + P].unsqueeze(2).to_broadcast([P, P, 4]),
                     op=ALU.add)
 
-        def quant_vp(n):
-            kind, b, g = seq[n]
-            lo = 512 * b
-            nc.vector.quantize_mx(out=pcod[:, lo : lo + 512].bitcast(FP8X4), scales=psca[:, lo : lo + 512],
-                                  in_=sm[("vg", b)][:])
+        def quant_vp(n, g=None):
+            kind, b, h = seq[n]
+            lo, wd, off = (512 * b, 512, 0) if g is None else (512 * b + 256 * g, 256, 1024 * g)
+            nc.vector.quantize_mx(out=pcod[:, lo : lo + wd].bitcast(FP8X4), scales=psca[:, lo : lo + wd],
+                                  in_=sm[("vg", b)][:, off : off + 4 * wd])
 
-        def passes_o(b):
+        def passes_o(b, cnt):
             ob = xtp.tile([P, 512], F32, name="ob", tag="xt")
-            for j in range(2):
+            for j in range(cnt):
                 for g in range(2):
                     mx(ob[:, DV * j : DV * j + DV], acod, asca, 1024 * g + P * (b + j), pcod, psca, 256 * (2 * (b + j) + g), DV, g)
             accs[("o", b)] = ob
 
-        def finish(b):
+        def finish(b, cnt):
             ot = otp.tile([P, 512], F32, name="ot", tag="ot")
-            if b % 4 == 2 and OUT_V:
-                nc.vector.tensor_copy(out=ot[:], in_=accs[("o", b)][:])
-            else:
-                nc.scalar.copy(out=ot[:], in_=accs[("o", b)][:])
-            nc.sync.dma_start(out=out[b : b + 2].rearrange("b i n -> i b n"), in_=ot[:].rearrange("p (b n) -> p b n", b=2))
+            w = DV * cnt
+            nc.scalar.copy(out=ot[:, 0:w], in_=accs[("o", b)][:, 0:w])
+            nc.sync.dma_start(out=out[b : b + cnt].rearrange("b i n -> i b n"), in_=ot[:, 0:w].rearrange("p (b n) -> p b n", b=cnt))
 
         def w_flip():
             words = wraw[:].bitcast(F32)
@@ -439,18 +446,22 @@ def tile_bottleneck_attention_pa_t_kernel(tc, qp_top, kp, v, Wv, bv, out):
                     else:
                         half_max(a, h)
                         if h == 1:
+                            if QSPLIT:
+                                quant(n + QLEAD, 0)
                             comb(a)
                     if h == 1:
+                        if QSPLIT:
+                            quant(n + QLEAD, 1)
                         sub(a, 0)
                         sub(a, 1)
                         if a % 2 == 1:
                             w = a // 2
-                            exps.extend([(w, x) for x in range(0, 4, EXPW)])
+                            exps.extend([(n + EXP_DELAY, w, x) for x in range(0, 4, EXPW)])
                 if kind == "v" and not is_b(m):
                     add_bias(m)
             if n + AHEAD == W_AT + 1:
                 w_quant()
-            if 0 <= n + QLEAD < N:
+            if 0 <= n + QLEAD < N and not (QSPLIT and 0 <= m < N and seq[m][0] == "k" and seq[m][2] == 1):
                 quant(n + QLEAD)
             if 0 <= n + AHEAD < N:
                 evac_v(n + AHEAD)
@@ -462,8 +473,8 @@ def tile_bottleneck_attention_pa_t_kernel(tc, qp_top, kp, v, Wv, bv, out):
             for f in waits.pop(("s", n), []):
                 f()
             for i in range(EXP_RATE // EXPW):
-                if exps:
-                    w, x = exps.pop(0)
+                if exps and exps[0][0] <= n:
+                    s, w, x = exps.pop(0)
                     expo(w, x)
                     if x == 4 - EXPW:
                         s = max(n + SUM_LAG, free_from)
@@ -486,7 +497,7 @@ def tile_bottleneck_attention_pa_t_kernel(tc, qp_top, kp, v, Wv, bv, out):
                                 waits.setdefault(("v", s + 1 + b // MUL_RATE), []).append(lambda g=g, b=b: mul(g, b))
                             if RB_COPY:
                                 free_from = s + 1
-                            s = s + 1 + B // MUL_RATE
+                            s = s + 1 + B // MUL_RATE + QA_LAG[g]
                             waits.setdefault(("v", s), []).append(lambda g=g: quant_attn(g))
                             if not RB_COPY:
                                 free_from = s
@@ -497,10 +508,15 @@ def tile_bottleneck_attention_pa_t_kernel(tc, qp_top, kp, v, Wv, bv, out):
                     continue
                 kind, b, g = seq[mm]
                 vdone.add((b, g))
-                if (b, 1 - g) in vdone:
+                if b == B - 1 and LASTQ:
+                    quant_vp(mm, g)
+                elif (b, 1 - g) in vdone:
                     quant_vp(mm)
-                if all((2 * (b // 2) + j, y) in vdone for j in range(2) for y in range(2)):
-                    ready_o.append(2 * (b // 2))
+                if LASTO and b >= B - 2:
+                    if (b, 1 - g) in vdone:
+                        ready_o.append((b, 1))
+                elif all((2 * (b // 2) + j, y) in vdone for j in range(2) for y in range(2)):
+                    ready_o.append((2 * (b // 2), 2))
             if 0 <= n < N:
                 if seq[n][0] == "k":
                     passes_k(n)
@@ -514,7 +530,7 @@ def tile_bottleneck_attention_pa_t_kernel(tc, qp_top, kp, v, Wv, bv, out):
             if attn_done:
                 for i in range(2):
                     if ready_o:
-                        b = ready_o.pop(0)
-                        passes_o(b)
-                        finish(b)
+                        b, cnt = ready_o.pop(0)
+                        passes_o(b, cnt)
+                        finish(b, cnt)
             n += 1

@@ -21,8 +21,8 @@ GRP = 3
 COD = 3
 AHEAD = 2
 QLEAD = 1
-W_AT = 10
-W_LOAD = 5
+W_AT = 14
+W_LOAD = 10
 WARM_0 = 8
 WARM_N = 1
 WARM_TO = 6
@@ -131,6 +131,11 @@ def tile_bottleneck_attention_pa_t_kernel(tc, qp_top, kp, v, Wv, bv, out):
                                   in_=src[:, w * i : w * i + w, :])
             raws[n] = raw
 
+        def load_w():
+            nc.sync.dma_start(out=wraw[:].rearrange("p (h d) -> p h d", h=2),
+                              in_=Wv.rearrange("(h p) d -> p h d", p=P))
+            nc.sync.dma_start(out=bias[:], in_=bv.partition_broadcast(P))
+
         def flip_slab(words, s, warm=0):
             xt = xtp.tile([P, 512], F32, name="xt", tag="xt")
             for i in range(warm):
@@ -157,6 +162,8 @@ def tile_bottleneck_attention_pa_t_kernel(tc, qp_top, kp, v, Wv, bv, out):
             xts[n] = [flip_slab(words, s, warm if s == 0 else 0) for s in range(4)]
             if n + RAW_BUFS < N:
                 load(n + RAW_BUFS)
+            if n + RAW_BUFS == W_LOAD:
+                load_w()
 
         def is_b(n):
             return 0 <= n < N and seq[n][0] == "v" and (seq[n][1], seq[n][2]) in BGRP
@@ -404,13 +411,8 @@ def tile_bottleneck_attention_pa_t_kernel(tc, qp_top, kp, v, Wv, bv, out):
         def w_quant():
             nc.vector.quantize_mx(out=wcod[:].bitcast(FP8X4), scales=wsca[:], in_=wgrp[:])
 
-        for n in range(-1, RAW_BUFS):
-            if n >= 0:
-                load(n)
-            if n == W_LOAD:
-                nc.sync.dma_start(out=wraw[:].rearrange("p (h d) -> p h d", h=2),
-                                  in_=Wv.rearrange("(h p) d -> p h d", p=P))
-                nc.sync.dma_start(out=bias[:], in_=bv.partition_broadcast(P))
+        for n in range(RAW_BUFS):
+            load(n)
 
         exps, peq, vq = [], [], []
         ready_o = []

@@ -21,8 +21,9 @@ GRP = 3
 COD = 3
 AHEAD = 2
 QLEAD = 1
-W_AT = 14
-W_LOAD = 10
+W_AT = 17
+W_LOAD = 14
+BIAS_LOAD = 17
 WARM_0 = 8
 WARM_N = 1
 WARM_TO = 6
@@ -134,7 +135,6 @@ def tile_bottleneck_attention_pa_t_kernel(tc, qp_top, kp, v, Wv, bv, out):
         def load_w():
             nc.sync.dma_start(out=wraw[:].rearrange("p (h d) -> p h d", h=2),
                               in_=Wv.rearrange("(h p) d -> p h d", p=P))
-            nc.sync.dma_start(out=bias[:], in_=bv.partition_broadcast(P))
 
         def flip_slab(words, s, warm=0):
             xt = xtp.tile([P, 512], F32, name="xt", tag="xt")
@@ -164,6 +164,8 @@ def tile_bottleneck_attention_pa_t_kernel(tc, qp_top, kp, v, Wv, bv, out):
                 load(n + RAW_BUFS)
             if n + RAW_BUFS == W_LOAD:
                 load_w()
+            if n + RAW_BUFS == BIAS_LOAD:
+                nc.sync.dma_start(out=bias[:], in_=bv.partition_broadcast(P))
 
         def is_b(n):
             return 0 <= n < N and seq[n][0] == "v" and (seq[n][1], seq[n][2]) in BGRP
@@ -434,6 +436,7 @@ def tile_bottleneck_attention_pa_t_kernel(tc, qp_top, kp, v, Wv, bv, out):
             if n + AHEAD == W_AT:
                 w_flip()
                 w_evac()
+            if n + AHEAD == W_AT + 3:
                 bias_columns()
             for f in waits.pop(("pe", n), []):
                 f()

@@ -36,7 +36,7 @@ MUL_RATE = 2
 MULB = 2
 EXP_DELAY = 1
 GPM = ()
-QA_LAG = (0, 0)
+QA_LAG = (1, 0)
 EXPW = 2
 QPAIR = 1
 QVP = 2
@@ -52,7 +52,7 @@ DD = 3
 EE = 2
 SPLIT = 2
 TAIL_VE = 0
-VE_MOD = 1
+VE_MOD = 2
 RCP_S = (0, 0)
 RCP_SPLIT = 1
 RB_COPY = 1
@@ -73,7 +73,7 @@ def tile_bottleneck_attention_pa_t_kernel(tc, qp_top, kp, v, Wv, bv, out):
         dep = ctx.enter_context(tc.tile_pool(name="dep", bufs=DD))
         smp = ctx.enter_context(tc.tile_pool(name="smp", bufs=2))
         vpp = ctx.enter_context(tc.tile_pool(name="vpp", bufs=3))
-        otp = ctx.enter_context(tc.tile_pool(name="otp", bufs=2))
+        otp = ctx.enter_context(tc.tile_pool(name="otp", bufs=3))
         xtp = ctx.enter_context(tc.psum_pool(name="xtp", bufs=XT))
         accp = ctx.enter_context(tc.psum_pool(name="accp", bufs=ACC))
         mscp = ctx.enter_context(tc.psum_pool(name="mscp", bufs=MSC))

@@ -24,11 +24,11 @@ QLEAD = 1
 W_AT = 17
 W_LOAD = 14
 BIAS_LOAD = 17
-WARM_0 = 8
+WARM_0 = 2
 WARM_N = 1
 WARM_TO = 6
 VE_FIRST = 4
-VE_LAST = 10
+VE_LAST = 14
 EXP_RATE = 2
 SUM_LAG = 1
 RCP_PIECES = 1
@@ -41,7 +41,7 @@ EXPW = 2
 QPAIR = 1
 QVP = 2
 QSPLIT = 1
-BGRP = ((1, 1), (2, 1), (3, 1), (4, 1), (5, 1))
+BGRP = ((1, 1), (2, 1), (3, 1), (4, 1), (6, 0))
 TVE = 0
 LASTQ = 1
 LASTO = 1

@@ -24,9 +24,9 @@ QLEAD = 1
 W_AT = 17
 W_LOAD = 14
 BIAS_LOAD = 17
-WARM_0 = 2
+WARM_0 = 0
 WARM_N = 1
-WARM_TO = 6
+WARM_TO = 0
 VE_FIRST = 4
 VE_LAST = 14
 EXP_RATE = 2

from contextlib import ExitStack

import concourse.mybir as mybir
from concourse.masks import make_identity

F32 = mybir.dt.float32
BF16 = mybir.dt.bfloat16
U32 = mybir.dt.uint32
U8 = mybir.dt.uint8
FP8X4 = mybir.dt.float8_e4m3fn_x4
ALU = mybir.AluOpType
ACT = mybir.ActivationFunctionType
AX = mybir.AxisListType

B, L, D, DV, BN = 8, 1024, 1024, 256, 128
P = 128
FLOPS = 2 * B * L * D * DV + 2 * B * BN * L * D + 2 * B * BN * L * DV

RAW_BUFS = 6
GRP = 3
COD = 3
AHEAD = 2
QLEAD = 1
W_AT = 17
W_LOAD = 14
BIAS_LOAD = 17
WARM_0 = 0
WARM_N = 1
WARM_TO = 0
VE_FIRST = 4
VE_LAST = 14
EXP_RATE = 2
SUM_LAG = 1
RCP_PIECES = 1
MUL_RATE = 2
MULB = 2
EXP_DELAY = 1
GPM = ()
QA_LAG = (1, 0)
EXPW = 2
QPAIR = 1
QVP = 2
QSPLIT = 1
BGRP = ((1, 1), (2, 1), (3, 1), (4, 1), (6, 0))
TVE = 0
LASTQ = 1
LASTO = 1
XT = 4
ACC = 3
MSC = 1
DD = 3
EE = 2
SPLIT = 2
TAIL_VE = 0
VE_MOD = 2
RCP_S = (0, 0)
RCP_SPLIT = 1
RB_COPY = 1
MLAG = 1
HELP = ()
VMIX = ()
VF = 0
VF2 = 0


def tile_bottleneck_attention_pa_t_kernel(tc, qp_top, kp, v, Wv, bv, out):
    nc = tc.nc
    with ExitStack() as ctx:
        const = ctx.enter_context(tc.tile_pool(name="const", bufs=1))
        rawp = ctx.enter_context(tc.tile_pool(name="rawp", bufs=RAW_BUFS))
        grpp = ctx.enter_context(tc.tile_pool(name="grpp", bufs=GRP))
        codp = ctx.enter_context(tc.tile_pool(name="codp", bufs=COD))
        dep = ctx.enter_context(tc.tile_pool(name="dep", bufs=DD))
        smp = ctx.enter_context(tc.tile_pool(name="smp", bufs=2))
        vpp = ctx.enter_context(tc.tile_pool(name="vpp", bufs=3))
        otp = ctx.enter_context(tc.tile_pool(name="otp", bufs=3))
        xtp = ctx.enter_context(tc.psum_pool(name="xtp", bufs=XT))
        accp = ctx.enter_context(tc.psum_pool(name="accp", bufs=ACC))
        mscp = ctx.enter_context(tc.psum_pool(name="mscp", bufs=MSC))
        ctx.enter_context(tc.manual_schedule())

        ident = const.tile([P, P], F32, name="ident")
        make_identity(nc, ident[:])
        qcod = const.tile([P, 2048], U32, name="qcod", align_bytes=64)
        qsca = const.tile([P, 2048], U8, name="qsca", align_bytes=64)
        wraw = const.tile([P, 2048], BF16, name="wraw")
        wgrp = const.tile([P, 2048], BF16, name="wgrp", align_bytes=64)
        wcod = const.tile([P, 512], U32, name="wcod", align_bytes=64)
        wsca = const.tile([P, 512], U8, name="wsca", align_bytes=64)
        bias = const.tile([P, DV], BF16, name="bias")
        biasf = const.tile([P, DV], F32, name="biasf")
        bcol = const.tile([P, 2], F32, name="bcol")
        pcod = const.tile([P, 4096], U32, name="pcod", align_bytes=64)
        psca = const.tile([P, 4096], U8, name="psca", align_bytes=64)
        acod = const.tile([P, 2048], U32, name="acod", align_bytes=64)
        asca = const.tile([P, 2048], U8, name="asca", align_bytes=64)
        ag = const.tile([P, 4096], BF16, name="ag", align_bytes=64)

        qview = qp_top.rearrange("b i d -> i b d")
        kview = kp.rearrange("b (g p t) d -> g t p b d", g=2, p=P, t=4)
        vview = v.rearrange("b (g p t) d -> b g p t d", g=2, p=P, t=4)

        vs = [("v", b, g) for b in range(B) for g in range(2)]
        seq = vs[:VF] + [("q", 0, 0), ("k", 0, 0)] + vs[VF:VF2] + [("q", 1, 0), ("k", 0, 1)]
        vi = VF2
        for u in range(1, 8):
            for h in range(2):
                seq.append(("k", u, h))
                if 2 * u + h in VMIX:
                    seq.append(vs[vi])
                    vi += 1
        seq.extend(vs[vi:])
        N = len(seq)

        raws, xts, grps, cods, scas, accs = {}, {}, {}, {}, {}, {}
        sm = {}

        def load(n):
            kind, a, h = seq[n]
            if kind == "q":
                src = qview[:, 4 * a : 4 * a + 4, :]
            elif kind == "k":
                src = kview[a // 4, a % 4][:, 4 * h : 4 * h + 4, :]
            else:
                src = vview[a, h]
            raw = rawp.tile([P, 4096], BF16, name="raw", tag="raw")
            dst = raw[:].rearrange("p (s d) -> p s d", s=4)
            pieces = 4 if n < SPLIT else 1
            w = 4 // pieces
            for i in range(pieces):
                nc.sync.dma_start(out=raw[:, 4096 // pieces * i : 4096 // pieces * (i + 1)].rearrange("p (s d) -> p s d", s=w),
                                  in_=src[:, w * i : w * i + w, :])
            raws[n] = raw

        def load_w():
            nc.sync.dma_start(out=wraw[:].rearrange("p (h d) -> p h d", h=2),
                              in_=Wv.rearrange("(h p) d -> p h d", p=P))

        def flip_slab(words, s, warm=0):
            xt = xtp.tile([P, 512], F32, name="xt", tag="xt")
            for i in range(warm):
                nc.tensor.matmul(out=xt[:, 0:P], lhsT=ident[:], rhs=ident[:], start=True, stop=True)
            for q in range(4):
                lo = 512 * s + 128 * q
                nc.tensor.transpose(xt[:, 128 * q : 128 * q + 128], words[:, lo : lo + 128], ident[:])
            return xt

        def evac_slab(eng_is_vector, gf, xt, s, wide=False):
            if wide:
                dst = gf.rearrange("p (c t r u) -> p t c r u", c=2, t=4, r=P, u=2)[:, s]
            else:
                dst = gf[:, 512 * s : 512 * s + 512].rearrange("p (c r u) -> p c r u", c=2, r=P, u=2)
            src = xt[:].rearrange("p (c u r) -> p c r u", c=2, u=2, r=P)
            if eng_is_vector:
                nc.vector.tensor_copy(out=dst, in_=src)
            else:
                nc.scalar.copy(out=dst, in_=src)

        def flip(n):
            words = raws[n][:].bitcast(F32)
            warm = WARM_0 if n == 0 else (WARM_N if n < WARM_TO else 0)
            xts[n] = [flip_slab(words, s, warm if s == 0 else 0) for s in range(4)]
            if n + RAW_BUFS < N:
                load(n + RAW_BUFS)
            if n + RAW_BUFS == W_LOAD:
                load_w()
            if n + RAW_BUFS == BIAS_LOAD:
                nc.sync.dma_start(out=bias[:], in_=bv.partition_broadcast(P))

        def is_b(n):
            return 0 <= n < N and seq[n][0] == "v" and (seq[n][1], seq[n][2]) in BGRP

        def vector_slabs(n):
            if n >= N - TAIL_VE:
                return (1, 3)
            if VE_FIRST <= n < VE_LAST and n % VE_MOD == VE_MOD - 1:
                return (3,)
            return ()

        def evac(n):
            grp = grpp.tile([P, 4096], BF16, name="grp", tag="grp", align_bytes=64)
            gf = grp[:].bitcast(F32)
            for s in range(4):
                if s not in vector_slabs(n):
                    evac_slab(False, gf, xts[n][s], s, is_b(n))
            grps[n] = grp

        def evac_v(n):
            gf = grps[n][:].bitcast(F32)
            for s in vector_slabs(n):
                evac_slab(True, gf, xts[n][s], s, is_b(n))

        def quant(n, part=None):
            kind, a, h = seq[n]
            if kind == "q":
                cod = qcod[:, 1024 * a : 1024 * a + 1024]
                sca = qsca[:, 1024 * a : 1024 * a + 1024]
            elif part != 1:
                codt = codp.tile([P, 1024], U32, name="codt", tag="codt", align_bytes=64)
                scat = codp.tile([P, 1024], U8, name="scat", tag="scat", align_bytes=64)
                cod = codt[:]
                sca = scat[:]
            else:
                cod = cods[n]
                sca = scas[n]
            cods[n] = cod
            scas[n] = sca
            lo, hi = (0, 1024) if part is None else (512 * part, 512 * part + 512)
            nc.vector.quantize_mx(out=cod[:, lo:hi].bitcast(FP8X4), scales=sca[:, lo:hi], in_=grps[n][:, 4 * lo : 4 * hi])

        def mx(acc, lc, ls, lo, rc, rs, ro, width, c):
            nc.tensor.matmul_mx(
                out=acc,
                lhsT=lc[:, lo : lo + P].bitcast(FP8X4),
                lhsT_scale=ls[:, lo : lo + P],
                rhs=rc[:, ro : ro + width].bitcast(FP8X4),
                rhs_scale=rs[:, ro : ro + width],
                start=(c == 0),
                stop=(c == 1),
            )

        def passes_k(n):
            kind, u, h = seq[n]
            sc = accp.tile([P, 512], F32, name="sc", tag="acc")
            for s in range(4):
                b = 4 * h + s
                for c in range(2):
                    mx(sc[:, P * s : P * s + P], cods[n], scas[n], (2 * s + c) * P,
                       qcod, qsca, (2 * b + c) * P, P, c)
            accs[("k", u, h)] = sc

        def passes_v(n):
            for h in range(2):
                vb = accp.tile([P, 512], F32, name="vb", tag="acc")
                for t in range(4):
                    for c in range(2):
                        mx(vb[:, P * t : P * t + P], cods[n], scas[n], (2 * t + c) * P,
                           wcod, wsca, (2 * h + c) * P, P, c)
                accs[("v", n, h)] = vb

        def passes_w(n):
            for h in range(2):
                vb = accp.tile([P, 512], F32, name="vb", tag="acc")
                for c in range(2):
                    mx(vb[:], wcod, wsca, (2 * h + c) * P, cods[n], scas[n], 512 * c, 512, c)
                accs[("v", n, h)] = vb

        def bias_s(n):
            vt = vpp.tile([P, 1024], BF16, name="vt", tag="vt", bufs=2)
            for h in range(2):
                nc.scalar.activation(
                    out=vt[:, 512 * h : 512 * h + 512].rearrange("p (a r t) -> p a r t", a=2, r=P, t=2),
                    in_=accs[("v", n, h)][:].rearrange("p (a t r) -> p a r t", a=2, t=2, r=P),
                    func=ACT.Identity, bias=bcol[:, h : h + 1])
            sm[("vt", n)] = vt

        def flip_vt(n):
            tv = accp.tile([P, 512], F32, name="tv", tag="acc")
            words = sm[("vt", n)][:].bitcast(F32)
            for q in range(4):
                nc.tensor.transpose(tv[:, P * q : P * q + P], words[:, P * q : P * q + P], ident[:])
            sm[("tv", n)] = tv

        def evac_vt(n):
            kind, b, g = seq[n]
            if ("vg", b) not in sm:
                sm[("vg", b)] = vpp.tile([P, 2048], BF16, name="vg", tag="vg", align_bytes=64)
            evac_slab(TVE, sm[("vg", b)][:, 1024 * g : 1024 * g + 1024].bitcast(F32), sm[("tv", n)], 0)

        def bias_columns():
            nc.vector.tensor_copy(out=biasf[:], in_=bias[:])
            xb = xtp.tile([P, 512], F32, name="xb", tag="xt")
            for h in range(2):
                nc.tensor.transpose(xb[:, P * h : P * h + P], biasf[:, P * h : P * h + P], ident[:])
            nc.scalar.copy(out=bcol[:], in_=xb[:, 0 : 2 * P].rearrange("p (h x) -> p h x", h=2)[:, :, 0])

        def half_max(u, h):
            mh = smp.tile([P, P], F32, name="mh%d" % h, tag="mh%d" % h)
            nc.vector.tensor_reduce(
                out=mh[:], in_=accs[("k", u, h)][:].rearrange("p (b i) -> p i b", b=4),
                axis=AX.X, op=ALU.max)
            sm[("mh", u, h)] = mh

        def help_copy(u):
            hc = smp.tile([P, 512], BF16, name="hc", tag="hc")
            nc.scalar.copy(out=hc[:], in_=accs[("k", u, 0)][:])
            sm[("hc", u)] = hc

        def help_max(u):
            m4 = smp.tile([P, 512], BF16, name="m4", tag="m4")
            nc.vector.tensor_tensor(out=m4[:], in0=accs[("k", u, 1)][:], in1=sm[("hc", u)][:], op=ALU.max)
            m2 = smp.tile([P, 256], BF16, name="m2", tag="m2")
            nc.vector.tensor_tensor(out=m2[:], in0=m4[:, 0:256], in1=m4[:, 256:512], op=ALU.max)
            m = smp.tile([P, P], F32, name="m", tag="m")
            nc.vector.tensor_tensor(out=m[:], in0=m2[:, 0:128], in1=m2[:, 128:256], op=ALU.max)
            sm[("m", u)] = m

        def comb(u):
            m = smp.tile([P, P], F32, name="m", tag="m")
            nc.vector.tensor_tensor(out=m[:], in0=sm[("mh", u, 0)][:], in1=sm[("mh", u, 1)][:], op=ALU.max)
            sm[("m", u)] = m

        def sub(u, h):
            if ("d", u // 2) not in sm:
                sm[("d", u // 2)] = dep.tile([P, 2048], F32, name="dd", tag="dd")
            lo = 1024 * (u % 2) + 512 * h
            nc.vector.tensor_tensor(
                out=sm[("d", u // 2)][:, lo : lo + 512].rearrange("p (b i) -> p b i", b=4),
                in0=accs[("k", u, h)][:].rearrange("p (b i) -> p b i", b=4),
                in1=sm[("m", u)][:].unsqueeze(1).to_broadcast([P, 4, P]),
                op=ALU.subtract)

        def expo(w, x):
            g = w // 2
            if ("e", g) not in sm:
                sm[("e", g)] = dep.tile([P, 4096], F32, name="ee", tag="ee", bufs=EE)
            lo = 2048 * (w % 2) + 512 * x
            nc.scalar.activation(
                out=sm[("e", g)][:, lo : lo + 512 * EXPW].rearrange("p (c t) -> p c t", t=2),
                in_=sm[("d", w)][:].rearrange("p (t c) -> p c t", t=2)[:, 256 * x : 256 * x + 256 * EXPW, :],
                func=ACT.Exp, scale=1.0 / 32.0)

        def sum_pe(w, k):
            g = w // 2
            if ("sb", g) not in sm:
                sm[("sb", g)] = mscp.tile([P, 512], F32, name="sb", tag="msc")
            sb = sm[("sb", g)]
            eg = sm[("e", g)]
            o = 256 * (w % 2) + P * k
            for b in range(B):
                lo = 2048 * (w % 2) + 256 * b + P * k
                nc.tensor.matmul(out=sb[:, o : o + P], lhsT=eg[:, lo : lo + P],
                                 rhs=ident[:], is_transpose=True, start=(b == 0), stop=(b == B - 1))

        def recip(g, x):
            if ("rt", g) not in sm:
                sm[("rt", g)] = smp.tile([P, 512], F32, name="rt", tag="rt")
            wd = 512 // RCP_PIECES
            nc.vector.reciprocal(out=sm[("rt", g)][:, wd * x : wd * x + wd], in_=sm[("sb", g)][:, wd * x : wd * x + wd])

        def recip_ln(g):
            sm[("lt", g)] = smp.tile([P, 512], F32, name="lt", tag="lt", bufs=1)
            nc.scalar.activation(out=sm[("lt", g)][:], in_=sm[("sb", g)][:], func=ACT.Ln)

        def recip_exp(g):
            lt = sm[("lt", g)]
            sm[("rt", g)] = smp.tile([P, 512], F32, name="rt", tag="rt")
            nc.scalar.activation(out=sm[("rt", g)][:], in_=lt[:], func=ACT.Exp, scale=-1.0)

        def back_pe(g):
            rb = mscp.tile([P, 512], F32, name="rb", tag="msc")
            for k in range(4):
                nc.tensor.transpose(rb[:, P * k : P * k + P], sm[("rt", g)][:, P * k : P * k + P], ident[:])
            if RB_COPY:
                rs = smp.tile([P, 512], F32, name="rs", tag="rs", bufs=1)
                nc.scalar.copy(out=rs[:].rearrange("p (i w t) -> p i w t", w=2, t=2),
                               in_=rb[:].rearrange("p (w i t) -> p i w t", w=2, t=2))
                rb = rs
            sm[("rb", g)] = rb

        def mul(g, b):
            nc.vector.tensor_tensor(
                out=ag[:, 512 * b : 512 * (b + MULB)].rearrange("p (b i w t) -> p b i w t", b=MULB, w=2, t=2),
                in0=sm[("e", g)][:].rearrange("p (w b i t) -> p b i w t", w=2, b=B, t=2)[:, b : b + MULB],
                in1=sm[("rb", g)][:].rearrange("p (i w t) -> p i w t", w=2, t=2).unsqueeze(1).to_broadcast([P, MULB, P, 2, 2]),
                op=ALU.mult)

        def quant_attn(g):
            nc.vector.quantize_mx(out=acod[:, 1024 * g : 1024 * g + 1024].bitcast(FP8X4),
                                  scales=asca[:, 1024 * g : 1024 * g + 1024], in_=ag[:])

        def add_bias(n):
            kind, b, g = seq[n]
            if ("vg", b) not in sm:
                sm[("vg", b)] = vpp.tile([P, 2048], BF16, name="vg", tag="vg", align_bytes=64)
            vg = sm[("vg", b)]
            for h in range(2):
                lo = 1024 * g + 512 * h
                nc.vector.tensor_tensor(
                    out=vg[:, lo : lo + 512].rearrange("p (n t) -> p n t", t=4),
                    in0=accs[("v", n, h)][:].rearrange("p (t n) -> p n t", t=4),
                    in1=bias[:, P * h : P * h + P].unsqueeze(2).to_broadcast([P, P, 4]),
                    op=ALU.add)

        def quant_vp(n, g=None):
            kind, b, h = seq[n]
            lo, wd, off = (512 * b, 512, 0) if g is None else (512 * b + 256 * g, 256, 1024 * g)
            nc.vector.quantize_mx(out=pcod[:, lo : lo + wd].bitcast(FP8X4), scales=psca[:, lo : lo + wd],
                                  in_=sm[("vg", b)][:, off : off + 4 * wd])

        def passes_o(b, cnt):
            ob = xtp.tile([P, 512], F32, name="ob", tag="xt")
            for j in range(cnt):
                for g in range(2):
                    mx(ob[:, DV * j : DV * j + DV], acod, asca, 1024 * g + P * (b + j), pcod, psca, 256 * (2 * (b + j) + g), DV, g)
            accs[("o", b)] = ob

        def finish(b, cnt):
            ot = otp.tile([P, 512], F32, name="ot", tag="ot")
            w = DV * cnt
            nc.scalar.copy(out=ot[:, 0:w], in_=accs[("o", b)][:, 0:w])
            nc.sync.dma_start(out=out[b : b + cnt].rearrange("b i n -> i b n"), in_=ot[:, 0:w].rearrange("p (b n) -> p b n", b=cnt))

        def w_flip():
            words = wraw[:].bitcast(F32)
            xts["w"] = [flip_slab(words, s) for s in range(2)]

        def w_evac():
            gf = wgrp[:].bitcast(F32)
            for s in range(2):
                evac_slab(False, gf, xts["w"][s], s)

        def w_quant():
            nc.vector.quantize_mx(out=wcod[:].bitcast(FP8X4), scales=wsca[:], in_=wgrp[:])

        for n in range(RAW_BUFS):
            load(n)

        exps, peq, vq = [], [], []
        ready_o = []
        attn_done = False
        vdone = set()
        n = -AHEAD
        waits = {}
        free_from = 0
        while n < N + 4 or exps or peq or vq or ready_o:
            m = n - 1
            if is_b(m):
                bias_s(m)
            if 0 <= n + AHEAD < N:
                flip(n + AHEAD)
                evac(n + AHEAD)
            if is_b(n - 2):
                flip_vt(n - 2)
                evac_vt(n - 2)
            if n + AHEAD == W_AT:
                w_flip()
                w_evac()
            if n + AHEAD == W_AT + 3:
                bias_columns()
            for f in waits.pop(("pe", n), []):
                f()
            if 0 <= m < N:
                kind, a, h = seq[m]
                if kind == "k":
                    if a in HELP:
                        if h == 0:
                            help_copy(a)
                        else:
                            help_max(a)
                    else:
                        half_max(a, h)
                        if h == 1:
                            if QSPLIT:
                                quant(n + QLEAD, 0)
                            comb(a)
                    if h == 1:
                        if QSPLIT:
                            quant(n + QLEAD, 1)
                        sub(a, 0)
                        sub(a, 1)
                        if a % 2 == 1:
                            w = a // 2
                            exps.extend([(n + EXP_DELAY, w, x) for x in range(0, 4, EXPW)])
                if kind == "v" and not is_b(m):
                    add_bias(m)
            if n + AHEAD == W_AT + 1:
                w_quant()
            if 0 <= n + QLEAD < N and not (QSPLIT and 0 <= m < N and seq[m][0] == "k" and seq[m][2] == 1):
                quant(n + QLEAD)
            if 0 <= n + AHEAD < N:
                evac_v(n + AHEAD)
            for f in waits.pop(("v", n), []):
                f()
            if vq:
                for f in vq.pop(0):
                    f()
            for f in waits.pop(("s", n), []):
                f()
            for i in range(EXP_RATE // EXPW):
                if exps and exps[0][0] <= n:
                    s, w, x = exps.pop(0)
                    expo(w, x)
                    if x == 4 - EXPW:
                        s = max(n + SUM_LAG, free_from)
                        for k in range(2):
                            waits.setdefault(("pe", s + k), []).append(lambda w=w, k=k: sum_pe(w, k))
                        free_from = s + 2
                        if w % 2 == 1:
                            g = w // 2
                            s = s + 2
                            if RCP_S[g]:
                                waits.setdefault(("s", s), []).append(lambda g=g: recip_ln(g))
                                waits.setdefault(("s", s + RCP_SPLIT), []).append(lambda g=g: recip_exp(g))
                                s = s + 1 + RCP_SPLIT
                            else:
                                for r in range(RCP_PIECES):
                                    waits.setdefault(("v", s + r), []).append(lambda g=g, r=r: recip(g, r))
                                s = s + RCP_PIECES + 1
                            waits.setdefault(("pe", s), []).append(lambda g=g: back_pe(g))
                            for b in range(0, B, MULB):
                                waits.setdefault(("v", s + 1 + b // MUL_RATE), []).append(lambda g=g, b=b: mul(g, b))
                            if RB_COPY:
                                free_from = s + 1
                            s = s + 1 + B // MUL_RATE + QA_LAG[g]
                            waits.setdefault(("v", s), []).append(lambda g=g: quant_attn(g))
                            if not RB_COPY:
                                free_from = s
                            if g == 1:
                                waits.setdefault(("o", s + 1), []).append(None)
            for mm in (n - 3, n - 2):
                if not (0 <= mm < N and seq[mm][0] == "v" and is_b(mm) == (mm == n - 3)):
                    continue
                kind, b, g = seq[mm]
                vdone.add((b, g))
                if b == B - 1 and LASTQ:
                    quant_vp(mm, g)
                elif (b, 1 - g) in vdone:
                    quant_vp(mm)
                if LASTO and b >= B - 2:
                    if (b, 1 - g) in vdone:
                        ready_o.append((b, 1))
                elif all((2 * (b // 2) + j, y) in vdone for j in range(2) for y in range(2)):
                    ready_o.append((2 * (b // 2), 2))
            if 0 <= n < N:
                if seq[n][0] == "k":
                    passes_k(n)
                if seq[n][0] == "v":
                    if is_b(n):
                        passes_w(n)
                    else:
                        passes_v(n)
            if waits.pop(("o", n), []):
                attn_done = True
            if attn_done:
                for i in range(2):
                    if ready_o:
                        b, cnt = ready_o.pop(0)
                        passes_o(b, cnt)
                        finish(b, cnt)
            n += 1
